import numpy as np
import ml_dtypes


def mxq(x, axis, fmt="e4m3"):
    dtype, down = {"e4m3": (ml_dtypes.float8_e4m3fn, 7), "e5m2": (ml_dtypes.float8_e5m2, 14)}[fmt]
    v = np.moveaxis(np.asarray(x, np.float32).astype(ml_dtypes.bfloat16).astype(np.float64), axis, -1)
    blocks = v.reshape(v.shape[:-1] + (-1, 32))
    amax = np.abs(blocks).max(-1, keepdims=True)
    byte = np.maximum(np.where(amax > 0, np.frexp(amax)[1] - 1 + 127, 0) - down, 1)
    scale = np.exp2(byte - 127.0)
    codes = (blocks / scale).astype(np.float32).astype(dtype).astype(np.float64)
    return np.moveaxis((codes * scale).reshape(v.shape), -1, axis)


WIDE = False


def mx_kscale(k):
    if not WIDE:
        return np.ones(k)
    levels = np.array([10, -10, 5, -5, 0])
    a = np.random.permutation(np.resize(levels, k // 512 * 4)).reshape(k // 512, 4)
    idx = np.arange(k)
    return np.exp2(a[idx // 512, idx % 128 // 32])


BF16 = ml_dtypes.bfloat16


def bf(x):
    return np.asarray(x, np.float32).astype(BF16)


def f64(x):
    return np.asarray(x).astype(np.float64)


B, C, H, W, O, K = 4, 1024, 32, 32, 128, 3
DIRS = [(0, 1), (1, 1), (1, 0), (1, -1), (0, -1), (-1, -1), (-1, 0), (-1, 1)]
DILATION = 1
CENTER = K // 2
PAD = CENTER * DILATION


def setup_inputs():
    s = mx_kscale(C)
    bound = np.sqrt(6.0 / (C * K))
    return {"x": bf(np.random.standard_normal((B, C, H, W)) * s[None, :, None, None]),
            "weight": bf(np.random.uniform(-bound, bound, (O, C, K)) / s[None, :, None])}


def reference(x, weight):
    xq = mxq(f64(x).reshape(B, C, H * W), 1, "e4m3")
    wq = mxq(f64(weight).transpose(2, 0, 1).reshape(K * O, C), 1, "e4m3")
    y = (wq @ xq).reshape(B, K, O, H, W)
    yp = np.pad(y, ((0, 0), (0, 0), (0, 0), (PAD, PAD), (PAD, PAD)))
    outs = []
    for dy, dx in DIRS:
        acc = np.zeros((B, O, H, W))
        for k in range(K):
            r0 = PAD + (k - CENTER) * DILATION * dy
            c0 = PAD + (k - CENTER) * DILATION * dx
            acc = acc + yp[:, k, :, r0: r0 + H, c0: c0 + W]
        outs.append(acc)
    return np.stack(outs, axis=2)

@@ -1,0 +1,187 @@
+from contextlib import ExitStack
+
+import concourse.mybir as mybir
+from concourse.masks import make_identity
+
+FP8X4 = mybir.dt.float8_e4m3fn_x4
+BF16 = mybir.dt.bfloat16
+F32 = mybir.dt.float32
+U32 = mybir.dt.uint32
+U8 = mybir.dt.uint8
+I32 = mybir.dt.int32
+ADD = mybir.AluOpType.add
+
+B, C, H, W, O, K = 4, 1024, 32, 32, 128, 3
+P = 128
+PASSES = 2
+DIRS = [(0, 1), (1, 1), (1, 0), (1, -1), (0, -1), (-1, -1), (-1, 0), (-1, 1)]
+FLOPS = 2 * K * O * C * B * H * W
+
+SLOT = 64
+NSLOT = 18
+COLS = SLOT * NSLOT
+
+PE_DIRS = (2, 6)
+V_DIRS = (0, 4)
+G_DIRS = (1, 3, 5, 7)
+V_REGROUP = ((0, 0, 0), (0, 1, 0), (0, 1, 1), (1, 0, 0))
+
+
+def tile_r8convf_pa_t_kernel(tc, x, weight, out):
+    nc = tc.nc
+    with ExitStack() as ctx:
+        keep = ctx.enter_context(tc.tile_pool(name="keep", bufs=1))
+        stage = ctx.enter_context(tc.tile_pool(name="stage", bufs=3))
+        outs = ctx.enter_context(tc.tile_pool(name="outs", bufs=12))
+        ps_y1 = ctx.enter_context(tc.psum_pool(name="ps_y1", bufs=4))
+        ps_ev = ctx.enter_context(tc.psum_pool(name="ps_ev", bufs=4))
+
+        codes = [keep.tile([P, PASSES, COLS], U32, name="codes%d" % b, align_bytes=64) for b in range(B)]
+        scal = [keep.tile([P, PASSES, COLS], U8, name="scal%d" % b, align_bytes=64) for b in range(B)]
+        y0pad = [keep.tile([P, H + 2, W + 2], F32, name="y0pad%d" % s) for s in range(2)]
+        y2pad = [keep.tile([P, H + 2, W + 2], F32, name="y2pad%d" % s) for s in range(2)]
+        raw = [[keep.tile([P, 4, H * W], BF16, name="raw%d_%d" % (b, g)) for g in range(PASSES)] for b in range(B)]
+        w_sb = keep.tile([P, C * K], BF16, name="w_sb")
+        wperm = [keep.tile([P, PASSES, 4, P], BF16, name="wperm%d" % k) for k in range(K)]
+        wg = keep.tile([P, K, PASSES, P, 4], BF16, name="wg", align_bytes=64)
+        wq = keep.tile([P, K, PASSES * P], U32, name="wq", align_bytes=64)
+        ws = keep.tile([P, K, PASSES * P], U8, name="ws", align_bytes=64)
+        ident = keep.tile([P, P], BF16, name="ident")
+
+        nc.sync.dma_start(out=w_sb[:], in_=weight.rearrange("o c k -> o (c k)"))
+        for b in range(B):
+            for g in range(PASSES):
+                nc.sync.dma_start(
+                    out=raw[b][g][:].rearrange("p j n -> p (j n)"),
+                    in_=x[b, 512 * g:512 * (g + 1), :, :].rearrange("(p j) h w -> p (j h w)", j=4),
+                )
+
+        make_identity(nc, ident[:])
+        for s in range(2):
+            nc.gpsimd.memset(y0pad[s][:], 0.0)
+            nc.gpsimd.memset(y2pad[s][:], 0.0)
+        for b in range(B):
+            for lo in (0, COLS - SLOT):
+                nc.vector.memset(codes[b][:, :, lo:lo + SLOT].bitcast(I32), 0)
+                nc.vector.memset(scal[b][:, :, lo:lo + SLOT].bitcast(I32), 0)
+
+        w_view = w_sb[:].rearrange("o (g p t k) -> o k g t p", g=PASSES, p=P, t=4, k=K)
+        for k in range(K):
+            if k == 1:
+                nc.scalar.copy(out=wperm[k][:], in_=w_view[:, k])
+            else:
+                nc.vector.tensor_copy(out=wperm[k][:], in_=w_view[:, k])
+        for k in range(K):
+            wt = ps_ev.tile([P, PASSES, 4, P], BF16, name="wt", tag="ev")
+            for g in range(PASSES):
+                for t in range(4):
+                    nc.tensor.transpose(wt[:, g, t, :], wperm[k][:, g, t, :], ident[:])
+            if k == 1:
+                nc.scalar.copy(out=wg[:, k], in_=wt[:].rearrange("p g t o -> p g o t"))
+            else:
+                nc.vector.tensor_copy(out=wg[:, k], in_=wt[:].rearrange("p g t o -> p g o t"))
+        for k in range(K):
+            nc.vector.quantize_mx(
+                out=wq[:, k, :].bitcast(FP8X4),
+                scales=ws[:, k, :],
+                in_=wg[:, k].rearrange("p g o t -> p (g o t)"),
+            )
+
+        def passes(acc, b, i, taps):
+            n = len(taps) * PASSES
+            j = 0
+            for k, s in taps:
+                c0 = SLOT * (1 + 8 * i + s)
+                for g in range(PASSES):
+                    nc.tensor.matmul_mx(
+                        out=acc[:].rearrange("p a f w -> p (a f w)"),
+                        lhsT=wq[:, k, P * g:P * (g + 1)].bitcast(FP8X4),
+                        lhsT_scale=ws[:, k, P * g:P * (g + 1)],
+                        rhs=codes[b][:, g, c0:c0 + 512].bitcast(FP8X4),
+                        rhs_scale=scal[b][:, g, c0:c0 + 512],
+                        start=(j == 0),
+                        stop=(j == n - 1),
+                    )
+                    j += 1
+
+        def rows(ap3, i):
+            return ap3.rearrange("p (f i a) w -> p i a f w", f=2, i=2, a=8)[:, i]
+
+        for b in range(B):
+            for g in range(PASSES):
+                grouped = stage.tile([P, 16, 2, W, 4], BF16, name="grouped", align_bytes=64)
+                for f in range(2):
+                    src = raw[b][g][:, :, 512 * f:512 * (f + 1)]
+                    dst = grouped[:, :, f, :, :]
+                    if (b, g, f) in V_REGROUP:
+                        nc.vector.tensor_copy(
+                            out=dst.rearrange("p a (c i) t -> p a c t i", i=4),
+                            in_=src.rearrange("p t (a c i) -> p a c t i", a=16, i=4),
+                        )
+                    else:
+                        nc.scalar.copy(out=dst, in_=src.rearrange("p t (a w) -> p a w t", a=16))
+                nc.vector.quantize_mx(
+                    out=codes[b][:, g, SLOT:SLOT + 1024].bitcast(FP8X4),
+                    scales=scal[b][:, g, SLOT:SLOT + 1024],
+                    in_=grouped[:].rearrange("p a f w t -> p (a f w t)"),
+                )
+            for t in (codes[b], scal[b]):
+                nc.vector.tensor_copy(
+                    out=t[:, :, 32:64].bitcast(I32), in_=t[:, :, SLOT * 16:SLOT * 16 + 32].bitcast(I32))
+                nc.vector.tensor_copy(
+                    out=t[:, :, SLOT * 17:SLOT * 17 + 32].bitcast(I32), in_=t[:, :, SLOT + 32:SLOT + 64].bitcast(I32))
+
+            y0p = y0pad[b % 2]
+            y2p = y2pad[b % 2]
+            for k, pad in ((0, y0p), (2, y2p)):
+                for i in range(2):
+                    acc = ps_ev.tile([P, 8, 2, W], F32, name="acc", tag="ev")
+                    passes(acc, b, i, [(k, 0)])
+                    nc.scalar.copy(out=rows(pad[:, 1:H + 1, 1:W + 1], i), in_=acc[:])
+            y1 = []
+            for i in range(2):
+                acc1 = ps_y1.tile([P, 8, 2, W], F32, name="acc1", tag="y1")
+                passes(acc1, b, i, [(1, 0)])
+                y1.append(acc1)
+
+            od = {}
+            for d in range(8):
+                od[d] = outs.tile([P, H, W], F32, name="od", tag="od")
+
+            def store(d):
+                nc.sync.dma_start(
+                    out=out[b, :, d, :, :].rearrange("o h w -> o (h w)"),
+                    in_=od[d][:].rearrange("p h w -> p (h w)"),
+                )
+
+            for d in G_DIRS:
+                dy, dx = DIRS[d]
+                nc.gpsimd.tensor_tensor(
+                    out=od[d][:],
+                    in0=y0p[:, 1 - dy:1 - dy + H, 1 - dx:1 - dx + W],
+                    in1=y2p[:, 1 + dy:1 + dy + H, 1 + dx:1 + dx + W],
+                    op=ADD,
+                )
+            for d in V_DIRS:
+                dy, dx = DIRS[d]
+                for i in range(2):
+                    nc.vector.tensor_tensor(
+                        out=rows(od[d][:], i),
+                        in0=y1[i][:],
+                        in1=rows(y0p[:, 1 - dy:1 - dy + H, 1 - dx:1 - dx + W], i),
+                        op=ADD,
+                    )
+                nc.vector.tensor_tensor(
+                    out=od[d][:], in0=od[d][:], in1=y2p[:, 1 + dy:1 + dy + H, 1 + dx:1 + dx + W], op=ADD)
+                store(d)
+            for d in PE_DIRS:
+                dy, dx = DIRS[d]
+                for i in range(2):
+                    acc = ps_ev.tile([P, 8, 2, W], F32, name="acc", tag="ev")
+                    passes(acc, b, i, [(1, 0), (0, -dy), (2, dy)])
+                    nc.scalar.copy(out=rows(od[d][:], i), in_=acc[:])
+                store(d)
+            for d in G_DIRS:
+                for i in range(2):
+                    nc.vector.tensor_tensor(out=rows(od[d][:], i), in0=y1[i][:], in1=rows(od[d][:], i), op=ADD)
+                store(d)

@@ -14,174 +14,256 @@ ADD = mybir.AluOpType.add
 B, C, H, W, O, K = 4, 1024, 32, 32, 128, 3
 P = 128
 PASSES = 2
+PIX = H * W
 DIRS = [(0, 1), (1, 1), (1, 0), (1, -1), (0, -1), (-1, -1), (-1, 0), (-1, 1)]
 FLOPS = 2 * K * O * C * B * H * W
 
-SLOT = 64
-NSLOT = 18
-COLS = SLOT * NSLOT
+LEAD = 64
+COLS = LEAD + PIX + 64
+TROWS = 16
+PIECE = 256
 
 PE_DIRS = (2, 6)
 V_DIRS = (0, 4)
 G_DIRS = (1, 3, 5, 7)
-V_REGROUP = ((0, 0, 0), (0, 1, 0), (0, 1, 1), (1, 0, 0))
+V_PIECES = (3, 2, 1, 0)
 
 
 def tile_r8convf_pa_t_kernel(tc, x, weight, out):
     nc = tc.nc
     with ExitStack() as ctx:
         keep = ctx.enter_context(tc.tile_pool(name="keep", bufs=1))
-        stage = ctx.enter_context(tc.tile_pool(name="stage", bufs=3))
+        raws = ctx.enter_context(tc.tile_pool(name="raws", bufs=6))
+        stage = ctx.enter_context(tc.tile_pool(name="stage", bufs=4))
         outs = ctx.enter_context(tc.tile_pool(name="outs", bufs=12))
         ps_y1 = ctx.enter_context(tc.psum_pool(name="ps_y1", bufs=4))
-        ps_ev = ctx.enter_context(tc.psum_pool(name="ps_ev", bufs=4))
+        ps_y2 = ctx.enter_context(tc.psum_pool(name="ps_y2", bufs=2))
+        ps_ev = ctx.enter_context(tc.psum_pool(name="ps_ev", bufs=2))
+        ctx.enter_context(tc.manual_schedule())
 
         codes = [keep.tile([P, PASSES, COLS], U32, name="codes%d" % b, align_bytes=64) for b in range(B)]
-        scal = [keep.tile([P, PASSES, COLS], U8, name="scal%d" % b, align_bytes=64) for b in range(B)]
+        sc_a = [keep.tile([P, PASSES, COLS], U8, name="sc_a%d" % b, align_bytes=64) for b in range(B)]
+        sc_b = [keep.tile([P, PASSES, COLS], U8, name="sc_b%d" % b, align_bytes=64) for b in range(B)]
         y0pad = [keep.tile([P, H + 2, W + 2], F32, name="y0pad%d" % s) for s in range(2)]
         y2pad = [keep.tile([P, H + 2, W + 2], F32, name="y2pad%d" % s) for s in range(2)]
-        raw = [[keep.tile([P, 4, H * W], BF16, name="raw%d_%d" % (b, g)) for g in range(PASSES)] for b in range(B)]
         w_sb = keep.tile([P, C * K], BF16, name="w_sb")
         wperm = [keep.tile([P, PASSES, 4, P], BF16, name="wperm%d" % k) for k in range(K)]
-        wg = keep.tile([P, K, PASSES, P, 4], BF16, name="wg", align_bytes=64)
-        wq = keep.tile([P, K, PASSES * P], U32, name="wq", align_bytes=64)
-        ws = keep.tile([P, K, PASSES * P], U8, name="ws", align_bytes=64)
+        wg = [keep.tile([P, PASSES, P, 4], BF16, name="wg%d" % k, align_bytes=64) for k in range(K)]
+        wq = [keep.tile([P, PASSES * P], U32, name="wq%d" % k, align_bytes=64) for k in range(K)]
+        ws = [keep.tile([P, PASSES * P], U8, name="ws%d" % k, align_bytes=64) for k in range(K)]
         ident = keep.tile([P, P], BF16, name="ident")
+        raw = {}
+        grouped = {}
 
-        nc.sync.dma_start(out=w_sb[:], in_=weight.rearrange("o c k -> o (c k)"))
-        for b in range(B):
+        def load(b):
             for g in range(PASSES):
+                raw[(b, g)] = raws.tile([P, 4, PIX], BF16, name="raw", tag="raw")
                 nc.sync.dma_start(
-                    out=raw[b][g][:].rearrange("p j n -> p (j n)"),
+                    out=raw[(b, g)][:].rearrange("p j n -> p (j n)"),
                     in_=x[b, 512 * g:512 * (g + 1), :, :].rearrange("(p j) h w -> p (j h w)", j=4),
                 )
 
+        nc.sync.dma_start(out=w_sb[:], in_=weight.rearrange("o c k -> o (c k)"))
+        for b in range(3):
+            load(b)
+
         make_identity(nc, ident[:])
+        for b in range(B):
+            for t in (codes[b], sc_a[b], sc_b[b]):
+                nc.vector.memset(t[:, :, 0:LEAD + 32].bitcast(I32), 0)
+                nc.vector.memset(t[:, :, LEAD + PIX:COLS].bitcast(I32), 0)
+
+        w_view = w_sb[:].rearrange("o (g p t k) -> o k g t p", g=PASSES, p=P, t=4, k=K)
+        nc.scalar.copy(out=wperm[0][:], in_=w_view[:, 0])
+        nc.vector.tensor_copy(out=wperm[2][:], in_=w_view[:, 2])
+        nc.scalar.copy(out=wperm[1][:], in_=w_view[:, 1])
+        wt = {}
+        for k in (0, 2, 1):
+            wt[k] = ps_y1.tile([P, PASSES, 4, P], BF16, name="wt", tag="y1")
+            for g in range(PASSES):
+                for t in range(4):
+                    nc.tensor.transpose(wt[k][:, g, t, :], wperm[k][:, g, t, :], ident[:])
         for s in range(2):
             nc.gpsimd.memset(y0pad[s][:], 0.0)
             nc.gpsimd.memset(y2pad[s][:], 0.0)
-        for b in range(B):
-            for lo in (0, COLS - SLOT):
-                nc.vector.memset(codes[b][:, :, lo:lo + SLOT].bitcast(I32), 0)
-                nc.vector.memset(scal[b][:, :, lo:lo + SLOT].bitcast(I32), 0)
 
-        w_view = w_sb[:].rearrange("o (g p t k) -> o k g t p", g=PASSES, p=P, t=4, k=K)
-        for k in range(K):
-            if k == 1:
-                nc.scalar.copy(out=wperm[k][:], in_=w_view[:, k])
-            else:
-                nc.vector.tensor_copy(out=wperm[k][:], in_=w_view[:, k])
-        for k in range(K):
-            wt = ps_ev.tile([P, PASSES, 4, P], BF16, name="wt", tag="ev")
-            for g in range(PASSES):
-                for t in range(4):
-                    nc.tensor.transpose(wt[:, g, t, :], wperm[k][:, g, t, :], ident[:])
-            if k == 1:
-                nc.scalar.copy(out=wg[:, k], in_=wt[:].rearrange("p g t o -> p g o t"))
-            else:
-                nc.vector.tensor_copy(out=wg[:, k], in_=wt[:].rearrange("p g t o -> p g o t"))
-        for k in range(K):
+        def w_out(k):
+            nc.scalar.copy(out=wg[k][:], in_=wt[k][:].rearrange("p g t o -> p g o t"))
+
+        def quant_w(k):
             nc.vector.quantize_mx(
-                out=wq[:, k, :].bitcast(FP8X4),
-                scales=ws[:, k, :],
-                in_=wg[:, k].rearrange("p g o t -> p (g o t)"),
+                out=wq[k][:].bitcast(FP8X4), scales=ws[k][:], in_=wg[k][:].rearrange("p g o t -> p (g o t)"))
+
+        def piece(engine_copy, b, g, q):
+            if (b, g) not in grouped:
+                grouped[(b, g)] = stage.tile([P, PIX, 4], BF16, name="grouped", tag="grouped", align_bytes=64)
+            lo = PIECE * q
+            engine_copy(
+                out=grouped[(b, g)][:, lo:lo + PIECE, :].rearrange("p (c i) t -> p c t i", i=4),
+                in_=raw[(b, g)][:, :, lo:lo + PIECE].rearrange("p t (c i) -> p c t i", i=4),
+            )
+
+        def vector_pieces(b, g):
+            for q in range(V_PIECES[b]):
+                piece(nc.vector.tensor_copy, b, g, q)
+
+        waiting = [(b, g, q) for b in range(B) for g in range(PASSES) for q in range(V_PIECES[b], 4)]
+
+        def fill(n):
+            for r in range(min(n, len(waiting))):
+                b, g, q = waiting.pop(0)
+                piece(nc.scalar.copy, b, g, q)
+
+        def flush(b, g):
+            while len(waiting) > 0 and (waiting[0][0], waiting[0][1]) <= (b, g):
+                fill(1)
+
+        def quant(b, g):
+            nc.vector.quantize_mx(
+                out=codes[b][:, g, LEAD:LEAD + PIX].bitcast(FP8X4),
+                scales=sc_a[b][:, g, LEAD:LEAD + PIX],
+                in_=grouped[(b, g)][:].rearrange("p n t -> p (n t)"),
+            )
+
+        def second_plane(b):
+            nc.vector.tensor_copy(
+                out=sc_b[b][:, :, LEAD + 32:LEAD + 32 + PIX].bitcast(I32),
+                in_=sc_a[b][:, :, LEAD:LEAD + PIX].bitcast(I32),
             )
 
         def passes(acc, b, i, taps):
             n = len(taps) * PASSES
             j = 0
             for k, s in taps:
-                c0 = SLOT * (1 + 8 * i + s)
+                c0 = LEAD + W * (TROWS * i + s)
                 for g in range(PASSES):
+                    if s == 0:
+                        plane = sc_a[b][:, g, c0:c0 + 512]
+                    else:
+                        plane = sc_b[b][:, g, c0 + 32:c0 + 32 + 512]
                     nc.tensor.matmul_mx(
-                        out=acc[:].rearrange("p a f w -> p (a f w)"),
-                        lhsT=wq[:, k, P * g:P * (g + 1)].bitcast(FP8X4),
-                        lhsT_scale=ws[:, k, P * g:P * (g + 1)],
+                        out=acc[:].rearrange("p h w -> p (h w)"),
+                        lhsT=wq[k][:, P * g:P * (g + 1)].bitcast(FP8X4),
+                        lhsT_scale=ws[k][:, P * g:P * (g + 1)],
                         rhs=codes[b][:, g, c0:c0 + 512].bitcast(FP8X4),
-                        rhs_scale=scal[b][:, g, c0:c0 + 512],
+                        rhs_scale=plane,
                         start=(j == 0),
                         stop=(j == n - 1),
                     )
                     j += 1
 
-        def rows(ap3, i):
-            return ap3.rearrange("p (f i a) w -> p i a f w", f=2, i=2, a=8)[:, i]
+        od = {}
+        y1 = {}
+        y2 = {}
 
-        for b in range(B):
-            for g in range(PASSES):
-                grouped = stage.tile([P, 16, 2, W, 4], BF16, name="grouped", align_bytes=64)
-                for f in range(2):
-                    src = raw[b][g][:, :, 512 * f:512 * (f + 1)]
-                    dst = grouped[:, :, f, :, :]
-                    if (b, g, f) in V_REGROUP:
-                        nc.vector.tensor_copy(
-                            out=dst.rearrange("p a (c i) t -> p a c t i", i=4),
-                            in_=src.rearrange("p t (a c i) -> p a c t i", a=16, i=4),
-                        )
-                    else:
-                        nc.scalar.copy(out=dst, in_=src.rearrange("p t (a w) -> p a w t", a=16))
-                nc.vector.quantize_mx(
-                    out=codes[b][:, g, SLOT:SLOT + 1024].bitcast(FP8X4),
-                    scales=scal[b][:, g, SLOT:SLOT + 1024],
-                    in_=grouped[:].rearrange("p a f w t -> p (a f w t)"),
-                )
-            for t in (codes[b], scal[b]):
-                nc.vector.tensor_copy(
-                    out=t[:, :, 32:64].bitcast(I32), in_=t[:, :, SLOT * 16:SLOT * 16 + 32].bitcast(I32))
-                nc.vector.tensor_copy(
-                    out=t[:, :, SLOT * 17:SLOT * 17 + 32].bitcast(I32), in_=t[:, :, SLOT + 32:SLOT + 64].bitcast(I32))
+        def new_od(b, d):
+            od[(b, d)] = outs.tile([P, H, W], F32, name="od", tag="od")
+            return od[(b, d)]
 
-            y0p = y0pad[b % 2]
-            y2p = y2pad[b % 2]
-            for k, pad in ((0, y0p), (2, y2p)):
+        def store(queue, b, d):
+            queue.dma_start(
+                out=out[b, :, d, :, :].rearrange("o h w -> o (h w)"),
+                in_=od[(b, d)][:].rearrange("p h w -> p (h w)"),
+            )
+
+        def mm_y(b):
+            for k, pad in ((0, y0pad[b % 2]), (2, y2pad[b % 2])):
                 for i in range(2):
-                    acc = ps_ev.tile([P, 8, 2, W], F32, name="acc", tag="ev")
+                    acc = ps_ev.tile([P, TROWS, W], F32, name="acc", tag="ev")
                     passes(acc, b, i, [(k, 0)])
-                    nc.scalar.copy(out=rows(pad[:, 1:H + 1, 1:W + 1], i), in_=acc[:])
-            y1 = []
+                    nc.scalar.copy(out=pad[:, 1 + TROWS * i:1 + TROWS * (i + 1), 1:W + 1], in_=acc[:])
             for i in range(2):
-                acc1 = ps_y1.tile([P, 8, 2, W], F32, name="acc1", tag="y1")
-                passes(acc1, b, i, [(1, 0)])
-                y1.append(acc1)
+                y1[(b, i)] = ps_y1.tile([P, TROWS, W], F32, name="acc1", tag="y1")
+                passes(y1[(b, i)], b, i, [(1, 0)])
+            for i in range(2):
+                y2[(b, i)] = ps_y2.tile([P, TROWS, W], F32, name="acc2", tag="y2")
+                passes(y2[(b, i)], b, i, [(2, 0)])
+            fill(3)
 
-            od = {}
-            for d in range(8):
-                od[d] = outs.tile([P, H, W], F32, name="od", tag="od")
+        def mm_d(b):
+            for d in PE_DIRS:
+                dy = DIRS[d][0]
+                t = new_od(b, d)
+                for i in range(2):
+                    acc = ps_ev.tile([P, TROWS, W], F32, name="acc", tag="ev")
+                    passes(acc, b, i, [(1, 0), (0, -dy), (2, dy)])
+                    nc.scalar.copy(out=t[:, TROWS * i:TROWS * (i + 1), :], in_=acc[:])
+                    if i == 1:
+                        store(nc.scalar, b, d)
+                    fill(1)
 
-            def store(d):
-                nc.sync.dma_start(
-                    out=out[b, :, d, :, :].rearrange("o h w -> o (h w)"),
-                    in_=od[d][:].rearrange("p h w -> p (h w)"),
-                )
-
+        def gsum(b):
             for d in G_DIRS:
                 dy, dx = DIRS[d]
                 nc.gpsimd.tensor_tensor(
-                    out=od[d][:],
-                    in0=y0p[:, 1 - dy:1 - dy + H, 1 - dx:1 - dx + W],
-                    in1=y2p[:, 1 + dy:1 + dy + H, 1 + dx:1 + dx + W],
+                    out=new_od(b, d)[:],
+                    in0=y0pad[b % 2][:, 1 - dy:1 - dy + H, 1 - dx:1 - dx + W],
+                    in1=y2pad[b % 2][:, 1 + dy:1 + dy + H, 1 + dx:1 + dx + W],
                     op=ADD,
                 )
+
+        def vdirs(b):
             for d in V_DIRS:
-                dy, dx = DIRS[d]
+                dx = DIRS[d][1]
+                t = new_od(b, d)
                 for i in range(2):
+                    r = TROWS * i
                     nc.vector.tensor_tensor(
-                        out=rows(od[d][:], i),
-                        in0=y1[i][:],
-                        in1=rows(y0p[:, 1 - dy:1 - dy + H, 1 - dx:1 - dx + W], i),
+                        out=t[:, r:r + TROWS, :],
+                        in0=y1[(b, i)][:],
+                        in1=y0pad[b % 2][:, 1 + r:1 + r + TROWS, 1 - dx:1 - dx + W],
                         op=ADD,
                     )
-                nc.vector.tensor_tensor(
-                    out=od[d][:], in0=od[d][:], in1=y2p[:, 1 + dy:1 + dy + H, 1 + dx:1 + dx + W], op=ADD)
-                store(d)
-            for d in PE_DIRS:
-                dy, dx = DIRS[d]
+                lo = max(0, -dx)
                 for i in range(2):
-                    acc = ps_ev.tile([P, 8, 2, W], F32, name="acc", tag="ev")
-                    passes(acc, b, i, [(1, 0), (0, -dy), (2, dy)])
-                    nc.scalar.copy(out=rows(od[d][:], i), in_=acc[:])
-                store(d)
+                    r = TROWS * i
+                    nc.vector.tensor_tensor(
+                        out=t[:, r:r + TROWS, lo:lo + W - 1],
+                        in0=y2[(b, i)][:, :, lo + dx:lo + dx + W - 1],
+                        in1=t[:, r:r + TROWS, lo:lo + W - 1],
+                        op=ADD,
+                    )
+                store(nc.sync, b, d)
+
+        def finals(b):
             for d in G_DIRS:
+                t = od[(b, d)]
                 for i in range(2):
-                    nc.vector.tensor_tensor(out=rows(od[d][:], i), in0=y1[i][:], in1=rows(od[d][:], i), op=ADD)
-                store(d)
+                    r = TROWS * i
+                    nc.vector.tensor_tensor(
+                        out=t[:, r:r + TROWS, :], in0=y1[(b, i)][:], in1=t[:, r:r + TROWS, :], op=ADD)
+                store(nc.sync, b, d)
+
+        vector_pieces(0, 0)
+        w_out(0)
+        flush(0, 0)
+        w_out(2)
+        vector_pieces(0, 1)
+        quant(0, 0)
+        flush(0, 1)
+        w_out(1)
+        load(3)
+        quant_w(0)
+        quant_w(2)
+        quant(0, 1)
+        quant_w(1)
+        second_plane(0)
+        mm_y(0)
+        vector_pieces(1, 0)
+        vector_pieces(1, 1)
+        mm_d(0)
+        for b in range(B):
+            gsum(b)
+            vdirs(b)
+            if b + 1 < B:
+                flush(b + 1, 1)
+                quant(b + 1, 0)
+                quant(b + 1, 1)
+                second_plane(b + 1)
+                if b + 2 < B:
+                    vector_pieces(b + 2, 0)
+                    vector_pieces(b + 2, 1)
+                mm_y(b + 1)
+            finals(b)
+            if b + 1 < B:
+                mm_d(b + 1)

@@ -18,15 +18,19 @@ PIX = H * W
 DIRS = [(0, 1), (1, 1), (1, 0), (1, -1), (0, -1), (-1, -1), (-1, 0), (-1, 1)]
 FLOPS = 2 * K * O * C * B * H * W
 
-LEAD = 64
-COLS = LEAD + PIX + 64
+GAP = 64
+PITCH = PIX + GAP
+NBLK = B * PASSES
+FLAT = NBLK * PITCH + GAP
 TROWS = 16
 PIECE = 256
+PW = 40
+PC = 4
 
 PE_DIRS = (2, 6)
 V_DIRS = (0, 4)
 G_DIRS = (1, 3, 5, 7)
-V_PIECES = (3, 2, 1, 0)
+V_PIECES = (((0, 1), (0, 1, 2, 3)), ((0, 1), (0, 1)), ((0,), (0,)), ((), ()))
 
 
 def tile_r8convf_pa_t_kernel(tc, x, weight, out):
@@ -41,13 +45,12 @@ def tile_r8convf_pa_t_kernel(tc, x, weight, out):
         ps_ev = ctx.enter_context(tc.psum_pool(name="ps_ev", bufs=2))
         ctx.enter_context(tc.manual_schedule())
 
-        codes = [keep.tile([P, PASSES, COLS], U32, name="codes%d" % b, align_bytes=64) for b in range(B)]
-        sc_a = [keep.tile([P, PASSES, COLS], U8, name="sc_a%d" % b, align_bytes=64) for b in range(B)]
-        sc_b = [keep.tile([P, PASSES, COLS], U8, name="sc_b%d" % b, align_bytes=64) for b in range(B)]
-        y0pad = [keep.tile([P, H + 2, W + 2], F32, name="y0pad%d" % s) for s in range(2)]
-        y2pad = [keep.tile([P, H + 2, W + 2], F32, name="y2pad%d" % s) for s in range(2)]
+        codes = keep.tile([P, FLAT], U32, name="codes", align_bytes=64)
+        sc_a = keep.tile([P, FLAT], U8, name="sc_a", align_bytes=64)
+        sc_b = keep.tile([P, FLAT], U8, name="sc_b", align_bytes=64)
+        y0pad = [keep.tile([P, H + 2, PW], F32, name="y0pad%d" % s, align_bytes=64) for s in range(2)]
+        y2pad = [keep.tile([P, H + 2, PW], F32, name="y2pad%d" % s, align_bytes=64) for s in range(2)]
         w_sb = keep.tile([P, C * K], BF16, name="w_sb")
-        wperm = [keep.tile([P, PASSES, 4, P], BF16, name="wperm%d" % k) for k in range(K)]
         wg = [keep.tile([P, PASSES, P, 4], BF16, name="wg%d" % k, align_bytes=64) for k in range(K)]
         wq = [keep.tile([P, PASSES * P], U32, name="wq%d" % k, align_bytes=64) for k in range(K)]
         ws = [keep.tile([P, PASSES * P], U8, name="ws%d" % k, align_bytes=64) for k in range(K)]
@@ -55,37 +58,43 @@ def tile_r8convf_pa_t_kernel(tc, x, weight, out):
         raw = {}
         grouped = {}
 
-        def load(b):
+        def base(b, g):
+            return (PASSES * b + g) * PITCH + GAP
+
+        def load_part(b, lo, n):
             for g in range(PASSES):
-                raw[(b, g)] = raws.tile([P, 4, PIX], BF16, name="raw", tag="raw")
+                if (b, g) not in raw:
+                    raw[(b, g)] = raws.tile([P, 4, PIX], BF16, name="raw", tag="raw")
                 nc.sync.dma_start(
-                    out=raw[(b, g)][:].rearrange("p j n -> p (j n)"),
-                    in_=x[b, 512 * g:512 * (g + 1), :, :].rearrange("(p j) h w -> p (j h w)", j=4),
+                    out=raw[(b, g)][:, :, lo:lo + n],
+                    in_=x[b, 512 * g:512 * (g + 1), :, :].rearrange("(p j) h w -> p j (h w)", j=4)[:, :, lo:lo + n],
                 )
 
+        def load(b, halves):
+            for h in range(halves):
+                load_part(b, h * (PIX // halves), PIX // halves)
+
         nc.sync.dma_start(out=w_sb[:], in_=weight.rearrange("o c k -> o (c k)"))
-        for b in range(3):
-            load(b)
+        load(0, 2)
+        load(1, 1)
+        load(2, 1)
 
         make_identity(nc, ident[:])
-        for b in range(B):
-            for t in (codes[b], sc_a[b], sc_b[b]):
-                nc.vector.memset(t[:, :, 0:LEAD + 32].bitcast(I32), 0)
-                nc.vector.memset(t[:, :, LEAD + PIX:COLS].bitcast(I32), 0)
+        nc.vector.memset(codes[:, 0:NBLK * PITCH].rearrange("p (n c) -> p n c", c=PITCH)[:, :, 0:GAP].bitcast(I32), 0)
+        nc.vector.memset(codes[:, NBLK * PITCH:FLAT].bitcast(I32), 0)
+        nc.vector.memset(sc_b[:, 32:32 + NBLK * PITCH].rearrange("p (n c) -> p n c", c=PITCH)[:, :, 0:GAP].bitcast(I32), 0)
+        nc.vector.memset(sc_b[:, 32 + NBLK * PITCH:FLAT].bitcast(I32), 0)
+        for t in y0pad + y2pad:
+            nc.gpsimd.memset(t[:, 0:H + 2:H + 1, :], 0.0)
+            nc.gpsimd.memset(t[:, :, PC - 1:PC + W + 1:W + 1], 0.0)
 
         w_view = w_sb[:].rearrange("o (g p t k) -> o k g t p", g=PASSES, p=P, t=4, k=K)
-        nc.scalar.copy(out=wperm[0][:], in_=w_view[:, 0])
-        nc.vector.tensor_copy(out=wperm[2][:], in_=w_view[:, 2])
-        nc.scalar.copy(out=wperm[1][:], in_=w_view[:, 1])
         wt = {}
         for k in (0, 2, 1):
             wt[k] = ps_y1.tile([P, PASSES, 4, P], BF16, name="wt", tag="y1")
             for g in range(PASSES):
                 for t in range(4):
-                    nc.tensor.transpose(wt[k][:, g, t, :], wperm[k][:, g, t, :], ident[:])
-        for s in range(2):
-            nc.gpsimd.memset(y0pad[s][:], 0.0)
-            nc.gpsimd.memset(y2pad[s][:], 0.0)
+                    nc.tensor.transpose(wt[k][:, g, t, :], w_view[:, k, g, t, :], ident[:])
 
         def w_out(k):
             nc.scalar.copy(out=wg[k][:], in_=wt[k][:].rearrange("p g t o -> p g o t"))
@@ -103,49 +112,73 @@ def tile_r8convf_pa_t_kernel(tc, x, weight, out):
                 in_=raw[(b, g)][:, :, lo:lo + PIECE].rearrange("p t (c i) -> p c t i", i=4),
             )
 
-        def vector_pieces(b, g):
-            for q in range(V_PIECES[b]):
-                piece(nc.vector.tensor_copy, b, g, q)
+        todo = {(b, g): [q for q in range(4)] for b in range(B) for g in range(PASSES)}
+        order = [(b, g) for b in range(B) for g in range(PASSES)]
 
-        waiting = [(b, g, q) for b in range(B) for g in range(PASSES) for q in range(V_PIECES[b], 4)]
+        def vp(b, g, q):
+            todo[(b, g)].remove(q)
+            piece(nc.vector.tensor_copy, b, g, q)
+
+        def sp(b, g, q):
+            todo[(b, g)].remove(q)
+            piece(nc.scalar.copy, b, g, q)
+
+        vshare = {(b, g): list(V_PIECES[b][g]) for b in range(B) for g in range(PASSES)}
+
+        def vector_pieces(b):
+            for g in range(PASSES):
+                for q in vshare[(b, g)]:
+                    vp(b, g, q)
+
+        def s_next():
+            for bg in order:
+                for q in todo[bg]:
+                    if q not in vshare[bg]:
+                        return (bg[0], bg[1], q)
+            return None
 
         def fill(n):
-            for r in range(min(n, len(waiting))):
-                b, g, q = waiting.pop(0)
-                piece(nc.scalar.copy, b, g, q)
+            for r in range(n):
+                nx = s_next()
+                if nx is not None:
+                    sp(nx[0], nx[1], nx[2])
 
-        def flush(b, g):
-            while len(waiting) > 0 and (waiting[0][0], waiting[0][1]) <= (b, g):
-                fill(1)
+        def flush(b):
+            nx = s_next()
+            while nx is not None and nx[0] <= b:
+                sp(nx[0], nx[1], nx[2])
+                nx = s_next()
 
-        def quant(b, g):
+        def quant(b, g, lo=0, n=PIX):
+            c0 = base(b, g) + lo
             nc.vector.quantize_mx(
-                out=codes[b][:, g, LEAD:LEAD + PIX].bitcast(FP8X4),
-                scales=sc_a[b][:, g, LEAD:LEAD + PIX],
-                in_=grouped[(b, g)][:].rearrange("p n t -> p (n t)"),
+                out=codes[:, c0:c0 + n].bitcast(FP8X4),
+                scales=sc_a[:, c0:c0 + n],
+                in_=grouped[(b, g)][:, lo:lo + n, :].rearrange("p n t -> p (n t)"),
             )
 
         def second_plane(b):
+            bs = base(b, 0) - GAP
             nc.vector.tensor_copy(
-                out=sc_b[b][:, :, LEAD + 32:LEAD + 32 + PIX].bitcast(I32),
-                in_=sc_a[b][:, :, LEAD:LEAD + PIX].bitcast(I32),
+                out=sc_b[:, bs + 32:bs + 32 + PASSES * PITCH].rearrange("p (g c) -> p g c", c=PITCH)[:, :, GAP:GAP + PIX].bitcast(I32),
+                in_=sc_a[:, bs:bs + PASSES * PITCH].rearrange("p (g c) -> p g c", c=PITCH)[:, :, GAP:GAP + PIX].bitcast(I32),
             )
 
         def passes(acc, b, i, taps):
             n = len(taps) * PASSES
             j = 0
             for k, s in taps:
-                c0 = LEAD + W * (TROWS * i + s)
                 for g in range(PASSES):
+                    c0 = base(b, g) + W * (TROWS * i + s)
                     if s == 0:
-                        plane = sc_a[b][:, g, c0:c0 + 512]
+                        plane = sc_a[:, c0:c0 + 512]
                     else:
-                        plane = sc_b[b][:, g, c0 + 32:c0 + 32 + 512]
+                        plane = sc_b[:, c0 + 32:c0 + 32 + 512]
                     nc.tensor.matmul_mx(
                         out=acc[:].rearrange("p h w -> p (h w)"),
                         lhsT=wq[k][:, P * g:P * (g + 1)].bitcast(FP8X4),
                         lhsT_scale=ws[k][:, P * g:P * (g + 1)],
-                        rhs=codes[b][:, g, c0:c0 + 512].bitcast(FP8X4),
+                        rhs=codes[:, c0:c0 + 512].bitcast(FP8X4),
                         rhs_scale=plane,
                         start=(j == 0),
                         stop=(j == n - 1),
@@ -166,21 +199,17 @@ def tile_r8convf_pa_t_kernel(tc, x, weight, out):
                 in_=od[(b, d)][:].rearrange("p h w -> p (h w)"),
             )
 
-        def mm_y(b):
-            for k, pad in ((0, y0pad[b % 2]), (2, y2pad[b % 2])):
-                for i in range(2):
-                    acc = ps_ev.tile([P, TROWS, W], F32, name="acc", tag="ev")
-                    passes(acc, b, i, [(k, 0)])
-                    nc.scalar.copy(out=pad[:, 1 + TROWS * i:1 + TROWS * (i + 1), 1:W + 1], in_=acc[:])
-            for i in range(2):
-                y1[(b, i)] = ps_y1.tile([P, TROWS, W], F32, name="acc1", tag="y1")
-                passes(y1[(b, i)], b, i, [(1, 0)])
-            for i in range(2):
-                y2[(b, i)] = ps_y2.tile([P, TROWS, W], F32, name="acc2", tag="y2")
-                passes(y2[(b, i)], b, i, [(2, 0)])
-            fill(3)
+        def mm_y_half(b, i):
+            acc = ps_ev.tile([P, TROWS, W], F32, name="acc", tag="ev")
+            passes(acc, b, i, [(0, 0)])
+            nc.scalar.copy(out=y0pad[b % 2][:, 1 + TROWS * i:1 + TROWS * (i + 1), PC:PC + W], in_=acc[:])
+            y1[(b, i)] = ps_y1.tile([P, TROWS, W], F32, name="acc1", tag="y1")
+            passes(y1[(b, i)], b, i, [(1, 0)])
+            y2[(b, i)] = ps_y2.tile([P, TROWS, W], F32, name="acc2", tag="y2")
+            passes(y2[(b, i)], b, i, [(2, 0)])
+            nc.scalar.copy(out=y2pad[b % 2][:, 1 + TROWS * i:1 + TROWS * (i + 1), PC:PC + W], in_=y2[(b, i)][:])
 
-        def mm_d(b):
+        def mm_d(b, nfill):
             for d in PE_DIRS:
                 dy = DIRS[d][0]
                 t = new_od(b, d)
@@ -190,80 +219,113 @@ def tile_r8convf_pa_t_kernel(tc, x, weight, out):
                     nc.scalar.copy(out=t[:, TROWS * i:TROWS * (i + 1), :], in_=acc[:])
                     if i == 1:
                         store(nc.scalar, b, d)
-                    fill(1)
+                    fill(nfill)
 
-        def gsum(b):
-            for d in G_DIRS:
-                dy, dx = DIRS[d]
+        def gsum(b, d):
+            dy, dx = DIRS[d]
+            t = od[(b, d)]
+            for i in range(2):
+                r = TROWS * i
                 nc.gpsimd.tensor_tensor(
-                    out=new_od(b, d)[:],
-                    in0=y0pad[b % 2][:, 1 - dy:1 - dy + H, 1 - dx:1 - dx + W],
-                    in1=y2pad[b % 2][:, 1 + dy:1 + dy + H, 1 + dx:1 + dx + W],
+                    out=t[:, r:r + TROWS, :],
+                    in0=y0pad[b % 2][:, 1 - dy + r:1 - dy + r + TROWS, PC - dx:PC - dx + W],
+                    in1=y2pad[b % 2][:, 1 + dy + r:1 + dy + r + TROWS, PC + dx:PC + dx + W],
                     op=ADD,
                 )
 
-        def vdirs(b):
-            for d in V_DIRS:
-                dx = DIRS[d][1]
-                t = new_od(b, d)
-                for i in range(2):
-                    r = TROWS * i
-                    nc.vector.tensor_tensor(
-                        out=t[:, r:r + TROWS, :],
-                        in0=y1[(b, i)][:],
-                        in1=y0pad[b % 2][:, 1 + r:1 + r + TROWS, 1 - dx:1 - dx + W],
-                        op=ADD,
-                    )
-                lo = max(0, -dx)
-                for i in range(2):
-                    r = TROWS * i
-                    nc.vector.tensor_tensor(
-                        out=t[:, r:r + TROWS, lo:lo + W - 1],
-                        in0=y2[(b, i)][:, :, lo + dx:lo + dx + W - 1],
-                        in1=t[:, r:r + TROWS, lo:lo + W - 1],
-                        op=ADD,
-                    )
-                store(nc.sync, b, d)
+        def vdir(b, d):
+            dx = DIRS[d][1]
+            t = new_od(b, d)
+            for i in range(2):
+                r = TROWS * i
+                nc.vector.tensor_tensor(
+                    out=t[:, r:r + TROWS, :],
+                    in0=y1[(b, i)][:],
+                    in1=y0pad[b % 2][:, 1 + r:1 + r + TROWS, PC - dx:PC - dx + W],
+                    op=ADD,
+                )
+            lo = max(0, -dx)
+            for i in range(2):
+                r = TROWS * i
+                nc.vector.tensor_tensor(
+                    out=t[:, r:r + TROWS, lo:lo + W - 1],
+                    in0=y2[(b, i)][:, :, lo + dx:lo + dx + W - 1],
+                    in1=t[:, r:r + TROWS, lo:lo + W - 1],
+                    op=ADD,
+                )
+            store(nc.sync, b, d)
 
-        def finals(b):
-            for d in G_DIRS:
-                t = od[(b, d)]
-                for i in range(2):
-                    r = TROWS * i
-                    nc.vector.tensor_tensor(
-                        out=t[:, r:r + TROWS, :], in0=y1[(b, i)][:], in1=t[:, r:r + TROWS, :], op=ADD)
-                store(nc.sync, b, d)
+        def final(b, d):
+            t = od[(b, d)]
+            for i in range(2):
+                r = TROWS * i
+                nc.vector.tensor_tensor(
+                    out=t[:, r:r + TROWS, :], in0=y1[(b, i)][:], in1=t[:, r:r + TROWS, :], op=ADD)
+            store(nc.sync, b, d)
 
-        vector_pieces(0, 0)
+        def gate(b, d):
+            new_od(b, d)
+            nc.vector.memset(od[(b, d)][:, 0, 0:1], 0.0)
+
+        vp(0, 0, 0)
+        vp(0, 0, 1)
         w_out(0)
-        flush(0, 0)
+        vp(0, 1, 0)
+        vp(0, 1, 1)
         w_out(2)
-        vector_pieces(0, 1)
-        quant(0, 0)
-        flush(0, 1)
+        quant(0, 0, 0, 512)
+        quant(0, 1, 0, 512)
         w_out(1)
-        load(3)
+        sp(0, 0, 2)
+        sp(0, 0, 3)
         quant_w(0)
-        quant_w(2)
-        quant(0, 1)
         quant_w(1)
+        quant_w(2)
+        mm_y_half(0, 0)
+        vp(0, 1, 2)
+        vp(0, 1, 3)
+        load(3, 1)
+        quant(0, 0, 512, 512)
+        quant(0, 1, 512, 512)
         second_plane(0)
-        mm_y(0)
-        vector_pieces(1, 0)
-        vector_pieces(1, 1)
-        mm_d(0)
+        fill(1)
+        mm_y_half(0, 1)
+        vector_pieces(1)
+        gate(0, 1)
+        mm_d(0, 1)
+        EXTRA = (3, 3, 0, 0)
+        MDFILL = (1, 1, 1, 1)
         for b in range(B):
-            gsum(b)
-            vdirs(b)
+            if b > 0:
+                new_od(b, 1)
+            new_od(b, 3)
+            gsum(b, 1)
+            gsum(b, 3)
+            vdir(b, 0)
+            vdir(b, 4)
+            if b > 0:
+                final(b - 1, 7)
             if b + 1 < B:
-                flush(b + 1, 1)
+                flush(b + 1)
+                fill(EXTRA[b])
                 quant(b + 1, 0)
                 quant(b + 1, 1)
                 second_plane(b + 1)
                 if b + 2 < B:
-                    vector_pieces(b + 2, 0)
-                    vector_pieces(b + 2, 1)
-                mm_y(b + 1)
-            finals(b)
+                    vector_pieces(b + 2)
             if b + 1 < B:
-                mm_d(b + 1)
+                gate(b, 5)
+            else:
+                new_od(b, 5)
+            new_od(b, 7)
+            gsum(b, 5)
+            gsum(b, 7)
+            if b + 1 < B:
+                mm_y_half(b + 1, 0)
+                mm_y_half(b + 1, 1)
+            final(b, 1)
+            final(b, 3)
+            final(b, 5)
+            if b + 1 < B:
+                mm_d(b + 1, MDFILL[b + 1])
+        final(B - 1, 7)

@@ -24,6 +24,7 @@ NBLK = B * PASSES
 FLAT = NBLK * PITCH + GAP
 TROWS = 16
 PIECE = 256
+RUN = 8
 PW = 40
 PC = 4
 
@@ -108,8 +109,8 @@ def tile_r8convf_pa_t_kernel(tc, x, weight, out):
                 grouped[(b, g)] = stage.tile([P, PIX, 4], BF16, name="grouped", tag="grouped", align_bytes=64)
             lo = PIECE * q
             engine_copy(
-                out=grouped[(b, g)][:, lo:lo + PIECE, :].rearrange("p (c i) t -> p c t i", i=4),
-                in_=raw[(b, g)][:, :, lo:lo + PIECE].rearrange("p t (c i) -> p c t i", i=4),
+                out=grouped[(b, g)][:, lo:lo + PIECE, :].rearrange("p (c i) t -> p c t i", i=RUN),
+                in_=raw[(b, g)][:, :, lo:lo + PIECE].rearrange("p t (c i) -> p c t i", i=RUN),
             )
 
         todo = {(b, g): [q for q in range(4)] for b in range(B) for g in range(PASSES)}

@@ -160,7 +160,8 @@ def tile_r8convf_pa_t_kernel(tc, x, weight, out):
 
         def second_plane(b):
             bs = base(b, 0) - GAP
-            nc.vector.tensor_copy(
+            mover = nc.vector.tensor_copy if b == 0 else nc.sync.dma_start
+            mover(
                 out=sc_b[:, bs + 32:bs + 32 + PASSES * PITCH].rearrange("p (g c) -> p g c", c=PITCH)[:, :, GAP:GAP + PIX].bitcast(I32),
                 in_=sc_a[:, bs:bs + PASSES * PITCH].rearrange("p (g c) -> p g c", c=PITCH)[:, :, GAP:GAP + PIX].bitcast(I32),
             )

@@ -226,14 +226,12 @@ def tile_r8convf_pa_t_kernel(tc, x, weight, out):
         def gsum(b, d):
             dy, dx = DIRS[d]
             t = od[(b, d)]
-            for i in range(2):
-                r = TROWS * i
-                nc.gpsimd.tensor_tensor(
-                    out=t[:, r:r + TROWS, :],
-                    in0=y0pad[b % 2][:, 1 - dy + r:1 - dy + r + TROWS, PC - dx:PC - dx + W],
-                    in1=y2pad[b % 2][:, 1 + dy + r:1 + dy + r + TROWS, PC + dx:PC + dx + W],
-                    op=ADD,
-                )
+            nc.gpsimd.tensor_tensor(
+                out=t[:],
+                in0=y0pad[b % 2][:, 1 - dy:1 - dy + H, PC - dx:PC - dx + W],
+                in1=y2pad[b % 2][:, 1 + dy:1 + dy + H, PC + dx:PC + dx + W],
+                op=ADD,
+            )
 
         def vdir(b, d):
             dx = DIRS[d][1]

@@ -293,7 +293,8 @@ def tile_r8convf_pa_t_kernel(tc, x, weight, out):
         vector_pieces(1)
         gate(0, 1)
         mm_d(0, 1)
-        EXTRA = (3, 3, 0, 0)
+        EXTRA = (2, 2, 0, 0)
+        AFTER = (0, 1, 1, 0)
         MDFILL = (1, 1, 1, 1)
         for b in range(B):
             if b > 0:
@@ -327,5 +328,6 @@ def tile_r8convf_pa_t_kernel(tc, x, weight, out):
             final(b, 3)
             final(b, 5)
             if b + 1 < B:
+                fill(AFTER[b + 1])
                 mm_d(b + 1, MDFILL[b + 1])
         final(B - 1, 7)

@@ -31,6 +31,7 @@ PC = 4
 PE_DIRS = (2, 6)
 V_DIRS = (0, 4)
 G_DIRS = (1, 3, 5, 7)
+PAIR = (1, 3)
 V_PIECES = (((0, 1), (0, 1, 2, 3)), ((0, 1), (0, 1)), ((0,), (0,)), ((), ()))
 
 
@@ -40,7 +41,8 @@ def tile_r8convf_pa_t_kernel(tc, x, weight, out):
         keep = ctx.enter_context(tc.tile_pool(name="keep", bufs=1))
         raws = ctx.enter_context(tc.tile_pool(name="raws", bufs=6))
         stage = ctx.enter_context(tc.tile_pool(name="stage", bufs=4))
-        outs = ctx.enter_context(tc.tile_pool(name="outs", bufs=12))
+        outs = ctx.enter_context(tc.tile_pool(name="outs", bufs=10))
+        pairs = ctx.enter_context(tc.tile_pool(name="pairs", bufs=3))
         ps_y1 = ctx.enter_context(tc.psum_pool(name="ps_y1", bufs=4))
         ps_y2 = ctx.enter_context(tc.psum_pool(name="ps_y2", bufs=2))
         ps_ev = ctx.enter_context(tc.psum_pool(name="ps_ev", bufs=2))
@@ -104,32 +106,33 @@ def tile_r8convf_pa_t_kernel(tc, x, weight, out):
             nc.vector.quantize_mx(
                 out=wq[k][:].bitcast(FP8X4), scales=ws[k][:], in_=wg[k][:].rearrange("p g o t -> p (g o t)"))
 
-        def piece(engine_copy, b, g, q):
+        def piece(engine_copy, b, g, q, n):
             if (b, g) not in grouped:
                 grouped[(b, g)] = stage.tile([P, PIX, 4], BF16, name="grouped", tag="grouped", align_bytes=64)
             lo = PIECE * q
             engine_copy(
-                out=grouped[(b, g)][:, lo:lo + PIECE, :].rearrange("p (c i) t -> p c t i", i=RUN),
-                in_=raw[(b, g)][:, :, lo:lo + PIECE].rearrange("p t (c i) -> p c t i", i=RUN),
+                out=grouped[(b, g)][:, lo:lo + PIECE * n, :].rearrange("p (c i) t -> p c t i", i=RUN),
+                in_=raw[(b, g)][:, :, lo:lo + PIECE * n].rearrange("p t (c i) -> p c t i", i=RUN),
             )
 
         todo = {(b, g): [q for q in range(4)] for b in range(B) for g in range(PASSES)}
         order = [(b, g) for b in range(B) for g in range(PASSES)]
 
-        def vp(b, g, q):
-            todo[(b, g)].remove(q)
-            piece(nc.vector.tensor_copy, b, g, q)
+        def vp(b, g, q, n):
+            for j in range(n):
+                todo[(b, g)].remove(q + j)
+            piece(nc.vector.tensor_copy, b, g, q, n)
 
         def sp(b, g, q):
             todo[(b, g)].remove(q)
-            piece(nc.scalar.copy, b, g, q)
+            piece(nc.scalar.copy, b, g, q, 1)
 
         vshare = {(b, g): list(V_PIECES[b][g]) for b in range(B) for g in range(PASSES)}
 
         def vector_pieces(b):
             for g in range(PASSES):
-                for q in vshare[(b, g)]:
-                    vp(b, g, q)
+                if len(vshare[(b, g)]) > 0:
+                    vp(b, g, vshare[(b, g)][0], len(vshare[(b, g)]))
 
         def s_next():
             for bg in order:
@@ -188,6 +191,7 @@ def tile_r8convf_pa_t_kernel(tc, x, weight, out):
                     j += 1
 
         od = {}
+        pair = {}
         y1 = {}
         y2 = {}
 
@@ -223,11 +227,13 @@ def tile_r8convf_pa_t_kernel(tc, x, weight, out):
                         store(nc.scalar, b, d)
                     fill(nfill)
 
+        def new_pair(b):
+            pair[b] = pairs.tile([P, 2, H, W], F32, name="pair", tag="pair")
+
         def gsum(b, d):
             dy, dx = DIRS[d]
-            t = od[(b, d)]
             nc.gpsimd.tensor_tensor(
-                out=t[:],
+                out=pair[b][:, d // 2, :, :] if d in PAIR else od[(b, d)][:],
                 in0=y0pad[b % 2][:, 1 - dy:1 - dy + H, PC - dx:PC - dx + W],
                 in1=y2pad[b % 2][:, 1 + dy:1 + dy + H, PC + dx:PC + dx + W],
                 op=ADD,
@@ -263,15 +269,28 @@ def tile_r8convf_pa_t_kernel(tc, x, weight, out):
                     out=t[:, r:r + TROWS, :], in0=y1[(b, i)][:], in1=t[:, r:r + TROWS, :], op=ADD)
             store(nc.sync, b, d)
 
+        def final_pair(b):
+            t = pair[b]
+            for i in range(2):
+                r = TROWS * i
+                nc.vector.tensor_tensor(
+                    out=t[:, :, r:r + TROWS, :],
+                    in0=y1[(b, i)][:].unsqueeze(1).to_broadcast([P, 2, TROWS, W]),
+                    in1=t[:, :, r:r + TROWS, :],
+                    op=ADD,
+                )
+            nc.sync.dma_start(
+                out=out[b, :, PAIR[0]:PAIR[1] + 1:2, :, :].rearrange("o d h w -> o d (h w)"),
+                in_=t[:].rearrange("p d h w -> p d (h w)"),
+            )
+
         def gate(b, d):
             new_od(b, d)
             nc.vector.memset(od[(b, d)][:, 0, 0:1], 0.0)
 
-        vp(0, 0, 0)
-        vp(0, 0, 1)
+        vp(0, 0, 0, 2)
         w_out(0)
-        vp(0, 1, 0)
-        vp(0, 1, 1)
+        vp(0, 1, 0, 2)
         w_out(2)
         quant(0, 0, 0, 512)
         quant(0, 1, 0, 512)
@@ -282,8 +301,7 @@ def tile_r8convf_pa_t_kernel(tc, x, weight, out):
         quant_w(1)
         quant_w(2)
         mm_y_half(0, 0)
-        vp(0, 1, 2)
-        vp(0, 1, 3)
+        vp(0, 1, 2, 2)
         load(3, 1)
         quant(0, 0, 512, 512)
         quant(0, 1, 512, 512)
@@ -291,15 +309,15 @@ def tile_r8convf_pa_t_kernel(tc, x, weight, out):
         fill(1)
         mm_y_half(0, 1)
         vector_pieces(1)
-        gate(0, 1)
+        new_pair(0)
+        nc.vector.memset(pair[0][:, 0, 0, 0:1], 0.0)
         mm_d(0, 1)
         EXTRA = (2, 2, 0, 0)
         AFTER = (0, 1, 1, 0)
         MDFILL = (1, 1, 1, 1)
         for b in range(B):
             if b > 0:
-                new_od(b, 1)
-            new_od(b, 3)
+                new_pair(b)
             gsum(b, 1)
             gsum(b, 3)
             vdir(b, 0)
@@ -324,8 +342,7 @@ def tile_r8convf_pa_t_kernel(tc, x, weight, out):
             if b + 1 < B:
                 mm_y_half(b + 1, 0)
                 mm_y_half(b + 1, 1)
-            final(b, 1)
-            final(b, 3)
+            final_pair(b)
             final(b, 5)
             if b + 1 < B:
                 fill(AFTER[b + 1])

@@ -223,8 +223,6 @@ def tile_r8convf_pa_t_kernel(tc, x, weight, out):
                     acc = ps_ev.tile([P, TROWS, W], F32, name="acc", tag="ev")
                     passes(acc, b, i, [(1, 0), (0, -dy), (2, dy)])
                     nc.scalar.copy(out=t[:, TROWS * i:TROWS * (i + 1), :], in_=acc[:])
-                    if i == 1:
-                        store(nc.scalar, b, d)
                     fill(nfill)
 
         def new_pair(b):
@@ -321,9 +319,11 @@ def tile_r8convf_pa_t_kernel(tc, x, weight, out):
             gsum(b, 1)
             gsum(b, 3)
             vdir(b, 0)
+            store(nc.sync, b, 2)
             vdir(b, 4)
             if b > 0:
                 final(b - 1, 7)
+            store(nc.sync, b, 6)
             if b + 1 < B:
                 flush(b + 1)
                 fill(EXTRA[b])

@@ -32,7 +32,7 @@ PE_DIRS = (2, 6)
 V_DIRS = (0, 4)
 G_DIRS = (1, 3, 5, 7)
 PAIR = (1, 3)
-V_PIECES = (((0, 1), (0, 1, 2, 3)), ((0, 1), (0, 1)), ((0,), (0,)), ((), ()))
+V_PIECES = (((0, 1), (0, 1, 2, 3)), ((0, 1), (0, 1)), ((0, 1), ()), ((), ()))
 
 
 def tile_r8convf_pa_t_kernel(tc, x, weight, out):
@@ -163,11 +163,12 @@ def tile_r8convf_pa_t_kernel(tc, x, weight, out):
 
         def second_plane(b):
             bs = base(b, 0) - GAP
-            mover = nc.vector.tensor_copy if b == 0 else nc.sync.dma_start
-            mover(
-                out=sc_b[:, bs + 32:bs + 32 + PASSES * PITCH].rearrange("p (g c) -> p g c", c=PITCH)[:, :, GAP:GAP + PIX].bitcast(I32),
-                in_=sc_a[:, bs:bs + PASSES * PITCH].rearrange("p (g c) -> p g c", c=PITCH)[:, :, GAP:GAP + PIX].bitcast(I32),
-            )
+            moves = [(nc.vector.tensor_copy, 0, P)] if b == 0 else [(nc.sync.dma_start, 32 * q, 32 * q + 4) for q in range(4)]
+            for mover, lo, hi in moves:
+                mover(
+                    out=sc_b[lo:hi, bs + 32:bs + 32 + PASSES * PITCH].rearrange("p (g c) -> p g c", c=PITCH)[:, :, GAP:GAP + PIX].bitcast(I32),
+                    in_=sc_a[lo:hi, bs:bs + PASSES * PITCH].rearrange("p (g c) -> p g c", c=PITCH)[:, :, GAP:GAP + PIX].bitcast(I32),
+                )
 
         def passes(acc, b, i, taps):
             n = len(taps) * PASSES
@@ -310,8 +311,8 @@ def tile_r8convf_pa_t_kernel(tc, x, weight, out):
         new_pair(0)
         nc.vector.memset(pair[0][:, 0, 0, 0:1], 0.0)
         mm_d(0, 1)
-        EXTRA = (2, 2, 0, 0)
-        AFTER = (0, 1, 1, 0)
+        EXTRA = (2, 1, 0, 0)
+        AFTER = (0, 2, 2, 0)
         MDFILL = (1, 1, 1, 1)
         for b in range(B):
             if b > 0:

@@ -24,7 +24,8 @@ NBLK = B * PASSES
 FLAT = NBLK * PITCH + GAP
 TROWS = 16
 PIECE = 256
-RUN = 8
+V_RUN = 8
+S_RUN = 4
 PW = 40
 PC = 4
 
@@ -106,13 +107,13 @@ def tile_r8convf_pa_t_kernel(tc, x, weight, out):
             nc.vector.quantize_mx(
                 out=wq[k][:].bitcast(FP8X4), scales=ws[k][:], in_=wg[k][:].rearrange("p g o t -> p (g o t)"))
 
-        def piece(engine_copy, b, g, q, n):
+        def piece(engine_copy, b, g, q, n, run):
             if (b, g) not in grouped:
                 grouped[(b, g)] = stage.tile([P, PIX, 4], BF16, name="grouped", tag="grouped", align_bytes=64)
             lo = PIECE * q
             engine_copy(
-                out=grouped[(b, g)][:, lo:lo + PIECE * n, :].rearrange("p (c i) t -> p c t i", i=RUN),
-                in_=raw[(b, g)][:, :, lo:lo + PIECE * n].rearrange("p t (c i) -> p c t i", i=RUN),
+                out=grouped[(b, g)][:, lo:lo + PIECE * n, :].rearrange("p (c i) t -> p c t i", i=run),
+                in_=raw[(b, g)][:, :, lo:lo + PIECE * n].rearrange("p t (c i) -> p c t i", i=run),
             )
 
         todo = {(b, g): [q for q in range(4)] for b in range(B) for g in range(PASSES)}
@@ -121,11 +122,11 @@ def tile_r8convf_pa_t_kernel(tc, x, weight, out):
         def vp(b, g, q, n):
             for j in range(n):
                 todo[(b, g)].remove(q + j)
-            piece(nc.vector.tensor_copy, b, g, q, n)
+            piece(nc.vector.tensor_copy, b, g, q, n, V_RUN)
 
         def sp(b, g, q):
             todo[(b, g)].remove(q)
-            piece(nc.scalar.copy, b, g, q, 1)
+            piece(nc.scalar.copy, b, g, q, 1, S_RUN)
 
         vshare = {(b, g): list(V_PIECES[b][g]) for b in range(B) for g in range(PASSES)}
 

@@ -24,8 +24,7 @@ NBLK = B * PASSES
 FLAT = NBLK * PITCH + GAP
 TROWS = 16
 PIECE = 256
-V_RUN = 8
-S_RUN = 4
+RUN = 4
 PW = 40
 PC = 4
 
@@ -42,7 +41,8 @@ def tile_r8convf_pa_t_kernel(tc, x, weight, out):
         keep = ctx.enter_context(tc.tile_pool(name="keep", bufs=1))
         raws = ctx.enter_context(tc.tile_pool(name="raws", bufs=6))
         stage = ctx.enter_context(tc.tile_pool(name="stage", bufs=4))
-        outs = ctx.enter_context(tc.tile_pool(name="outs", bufs=10))
+        heads = ctx.enter_context(tc.tile_pool(name="heads", bufs=1))
+        outs = ctx.enter_context(tc.tile_pool(name="outs", bufs=7))
         pairs = ctx.enter_context(tc.tile_pool(name="pairs", bufs=3))
         ps_y1 = ctx.enter_context(tc.psum_pool(name="ps_y1", bufs=4))
         ps_y2 = ctx.enter_context(tc.psum_pool(name="ps_y2", bufs=2))
@@ -67,10 +67,14 @@ def tile_r8convf_pa_t_kernel(tc, x, weight, out):
 
         def load_part(b, lo, n):
             for g in range(PASSES):
-                if (b, g) not in raw:
+                if b == 0:
+                    raw[(b, g, lo)] = heads.tile([P, 4, n], BF16, name="head", tag="head%d%d" % (g, lo))
+                    dst = raw[(b, g, lo)][:]
+                else:
                     raw[(b, g)] = raws.tile([P, 4, PIX], BF16, name="raw", tag="raw")
+                    dst = raw[(b, g)][:]
                 nc.sync.dma_start(
-                    out=raw[(b, g)][:, :, lo:lo + n],
+                    out=dst,
                     in_=x[b, 512 * g:512 * (g + 1), :, :].rearrange("(p j) h w -> p j (h w)", j=4)[:, :, lo:lo + n],
                 )
 
@@ -82,6 +86,7 @@ def tile_r8convf_pa_t_kernel(tc, x, weight, out):
         load(0, 2)
         load(1, 1)
         load(2, 1)
+        load(3, 1)
 
         make_identity(nc, ident[:])
         nc.vector.memset(codes[:, 0:NBLK * PITCH].rearrange("p (n c) -> p n c", c=PITCH)[:, :, 0:GAP].bitcast(I32), 0)
@@ -107,13 +112,18 @@ def tile_r8convf_pa_t_kernel(tc, x, weight, out):
             nc.vector.quantize_mx(
                 out=wq[k][:].bitcast(FP8X4), scales=ws[k][:], in_=wg[k][:].rearrange("p g o t -> p (g o t)"))
 
-        def piece(engine_copy, b, g, q, n, run):
+        def piece(engine_copy, b, g, q, n):
             if (b, g) not in grouped:
                 grouped[(b, g)] = stage.tile([P, PIX, 4], BF16, name="grouped", tag="grouped", align_bytes=64)
             lo = PIECE * q
+            if b == 0:
+                first = lo // (PIX // 2) * (PIX // 2)
+                src = raw[(b, g, first)][:, :, lo - first:lo - first + PIECE * n]
+            else:
+                src = raw[(b, g)][:, :, lo:lo + PIECE * n]
             engine_copy(
-                out=grouped[(b, g)][:, lo:lo + PIECE * n, :].rearrange("p (c i) t -> p c t i", i=run),
-                in_=raw[(b, g)][:, :, lo:lo + PIECE * n].rearrange("p t (c i) -> p c t i", i=run),
+                out=grouped[(b, g)][:, lo:lo + PIECE * n, :].rearrange("p (c i) t -> p c t i", i=RUN),
+                in_=src.rearrange("p t (c i) -> p c t i", i=RUN),
             )
 
         todo = {(b, g): [q for q in range(4)] for b in range(B) for g in range(PASSES)}
@@ -122,11 +132,11 @@ def tile_r8convf_pa_t_kernel(tc, x, weight, out):
         def vp(b, g, q, n):
             for j in range(n):
                 todo[(b, g)].remove(q + j)
-            piece(nc.vector.tensor_copy, b, g, q, n, V_RUN)
+            piece(nc.vector.tensor_copy, b, g, q, n)
 
         def sp(b, g, q):
             todo[(b, g)].remove(q)
-            piece(nc.scalar.copy, b, g, q, 1, S_RUN)
+            piece(nc.scalar.copy, b, g, q, 1)
 
         vshare = {(b, g): list(V_PIECES[b][g]) for b in range(B) for g in range(PASSES)}
 
@@ -302,7 +312,6 @@ def tile_r8convf_pa_t_kernel(tc, x, weight, out):
         quant_w(2)
         mm_y_half(0, 0)
         vp(0, 1, 2, 2)
-        load(3, 1)
         quant(0, 0, 512, 512)
         quant(0, 1, 512, 512)
         second_plane(0)

@@ -40,7 +40,7 @@ def tile_r8convf_pa_t_kernel(tc, x, weight, out):
     with ExitStack() as ctx:
         keep = ctx.enter_context(tc.tile_pool(name="keep", bufs=1))
         raws = ctx.enter_context(tc.tile_pool(name="raws", bufs=6))
-        stage = ctx.enter_context(tc.tile_pool(name="stage", bufs=4))
+        stage = ctx.enter_context(tc.tile_pool(name="stage", bufs=1))
         heads = ctx.enter_context(tc.tile_pool(name="heads", bufs=1))
         outs = ctx.enter_context(tc.tile_pool(name="outs", bufs=7))
         pairs = ctx.enter_context(tc.tile_pool(name="pairs", bufs=3))
@@ -65,8 +65,8 @@ def tile_r8convf_pa_t_kernel(tc, x, weight, out):
         def base(b, g):
             return (PASSES * b + g) * PITCH + GAP
 
-        def load_part(b, lo, n):
-            for g in range(PASSES):
+        def load_part(b, lo, n, gs=(0, 1)):
+            for g in gs:
                 if b == 0:
                     raw[(b, g, lo)] = heads.tile([P, 4, n], BF16, name="head", tag="head%d%d" % (g, lo))
                     dst = raw[(b, g, lo)][:]
@@ -82,8 +82,12 @@ def tile_r8convf_pa_t_kernel(tc, x, weight, out):
             for h in range(halves):
                 load_part(b, h * (PIX // halves), PIX // halves)
 
-        nc.sync.dma_start(out=w_sb[:], in_=weight.rearrange("o c k -> o (c k)"))
-        load(0, 2)
+        for g in range(PASSES):
+            nc.sync.dma_start(
+                out=w_sb[:, C * K // 2 * g:C * K // 2 * (g + 1)],
+                in_=weight[:, C // 2 * g:C // 2 * (g + 1), :].rearrange("o c k -> o (c k)"))
+            load_part(0, 0, PIX // 2, (g,))
+        load_part(0, PIX // 2, PIX // 2)
         load(1, 1)
         load(2, 1)
         load(3, 1)
@@ -99,14 +103,15 @@ def tile_r8convf_pa_t_kernel(tc, x, weight, out):
 
         w_view = w_sb[:].rearrange("o (g p t k) -> o k g t p", g=PASSES, p=P, t=4, k=K)
         wt = {}
-        for k in (0, 2, 1):
-            wt[k] = ps_y1.tile([P, PASSES, 4, P], BF16, name="wt", tag="y1")
-            for g in range(PASSES):
+        for g in range(PASSES):
+            for k in (0, 2, 1):
+                pool, tag = (ps_y1, "y1") if g == 0 or k == 0 else (ps_ev, "ev")
+                wt[(k, g)] = pool.tile([P, 4, P], BF16, name="wt", tag=tag)
                 for t in range(4):
-                    nc.tensor.transpose(wt[k][:, g, t, :], w_view[:, k, g, t, :], ident[:])
+                    nc.tensor.transpose(wt[(k, g)][:, t, :], w_view[:, k, g, t, :], ident[:])
 
-        def w_out(k):
-            nc.scalar.copy(out=wg[k][:], in_=wt[k][:].rearrange("p g t o -> p g o t"))
+        def w_out(k, g):
+            nc.scalar.copy(out=wg[k][:, g, :, :], in_=wt[(k, g)][:].rearrange("p t o -> p o t"))
 
         def quant_w(k):
             nc.vector.quantize_mx(
@@ -114,7 +119,7 @@ def tile_r8convf_pa_t_kernel(tc, x, weight, out):
 
         def piece(engine_copy, b, g, q, n):
             if (b, g) not in grouped:
-                grouped[(b, g)] = stage.tile([P, PIX, 4], BF16, name="grouped", tag="grouped", align_bytes=64)
+                grouped[(b, g)] = stage.tile([P, PIX, 4], BF16, name="grouped", tag="s%d%d" % (b % 2, g), align_bytes=64)
             lo = PIECE * q
             if b == 0:
                 first = lo // (PIX // 2) * (PIX // 2)
@@ -237,50 +242,71 @@ def tile_r8convf_pa_t_kernel(tc, x, weight, out):
                     nc.scalar.copy(out=t[:, TROWS * i:TROWS * (i + 1), :], in_=acc[:])
                     fill(nfill)
 
-        def new_pair(b):
-            pair[b] = pairs.tile([P, 2, H, W], F32, name="pair", tag="pair")
+        def new_pair(b, first):
+            if first == 5 and b + 1 < B:
+                pair[(b, first)] = stage.tile([P, 2, H, W], F32, name="late", tag="s%d1" % ((b + 1) % 2), align_bytes=64)
+            else:
+                pair[(b, first)] = pairs.tile([P, 2, H, W], F32, name="pair", tag="pair")
 
         def gsum(b, d):
             dy, dx = DIRS[d]
             nc.gpsimd.tensor_tensor(
-                out=pair[b][:, d // 2, :, :] if d in PAIR else od[(b, d)][:],
+                out=pair[(b, 1 + d // 4 * 4)][:, d // 2 % 2, :, :],
                 in0=y0pad[b % 2][:, 1 - dy:1 - dy + H, PC - dx:PC - dx + W],
                 in1=y2pad[b % 2][:, 1 + dy:1 + dy + H, PC + dx:PC + dx + W],
                 op=ADD,
             )
 
-        def vdir(b, d):
+        def first_add(b, d, i):
+            r = TROWS * i
             dx = DIRS[d][1]
-            t = new_od(b, d)
+            nc.vector.tensor_tensor(
+                out=od[(b, d)][:, r:r + TROWS, :],
+                in0=y1[(b, i)][:],
+                in1=y0pad[b % 2][:, 1 + r:1 + r + TROWS, PC - dx:PC - dx + W],
+                op=ADD,
+            )
+
+        def second_add(b, d, i):
+            r = TROWS * i
+            dx = DIRS[d][1]
+            lo = max(0, -dx)
+            t = od[(b, d)][:, r:r + TROWS, lo:lo + W - 1]
+            nc.vector.tensor_tensor(out=t, in0=y2[(b, i)][:, :, lo + dx:lo + dx + W - 1], in1=t, op=ADD)
+
+        def vseven(b):
+            dy, dx = DIRS[7]
+            t = new_od(b, 7)
             for i in range(2):
                 r = TROWS * i
                 nc.vector.tensor_tensor(
                     out=t[:, r:r + TROWS, :],
                     in0=y1[(b, i)][:],
-                    in1=y0pad[b % 2][:, 1 + r:1 + r + TROWS, PC - dx:PC - dx + W],
+                    in1=y0pad[b % 2][:, 1 + r - dy:1 + r - dy + TROWS, PC - dx:PC - dx + W],
                     op=ADD,
                 )
-            lo = max(0, -dx)
             for i in range(2):
-                r = TROWS * i
-                nc.vector.tensor_tensor(
-                    out=t[:, r:r + TROWS, lo:lo + W - 1],
-                    in0=y2[(b, i)][:, :, lo + dx:lo + dx + W - 1],
-                    in1=t[:, r:r + TROWS, lo:lo + W - 1],
-                    op=ADD,
-                )
-            store(nc.sync, b, d)
+                r = TROWS * i + 1
+                n = min(TROWS, H - r)
+                part = t[:, r:r + n, 0:W - 1]
+                nc.vector.tensor_tensor(out=part, in0=y2[(b, i)][:, 0:n, 1:W], in1=part, op=ADD)
+            store(nc.sync, b, 7)
 
-        def final(b, d):
-            t = od[(b, d)]
+        def final(b, d, stores=1):
+            t = pair[(b, 1 + d // 4 * 4)][:, d // 2 % 2, :, :]
+            rows = H // stores
             for i in range(2):
                 r = TROWS * i
                 nc.vector.tensor_tensor(
                     out=t[:, r:r + TROWS, :], in0=y1[(b, i)][:], in1=t[:, r:r + TROWS, :], op=ADD)
-            store(nc.sync, b, d)
+                if (i + 1) * TROWS % rows == 0:
+                    r = (i + 1) * TROWS - rows
+                    nc.sync.dma_start(
+                        out=out[b, :, d, r:r + rows, :].rearrange("o h w -> o (h w)"),
+                        in_=t[:, r:r + rows, :].rearrange("p h w -> p (h w)"))
 
         def final_pair(b):
-            t = pair[b]
+            t = pair[(b, 1)]
             for i in range(2):
                 r = TROWS * i
                 nc.vector.tensor_tensor(
@@ -294,17 +320,11 @@ def tile_r8convf_pa_t_kernel(tc, x, weight, out):
                 in_=t[:].rearrange("p d h w -> p d (h w)"),
             )
 
-        def gate(b, d):
-            new_od(b, d)
-            nc.vector.memset(od[(b, d)][:, 0, 0:1], 0.0)
-
-        vp(0, 0, 0, 2)
-        w_out(0)
-        vp(0, 1, 0, 2)
-        w_out(2)
-        quant(0, 0, 0, 512)
-        quant(0, 1, 0, 512)
-        w_out(1)
+        for g in range(PASSES):
+            vp(0, g, 0, 2)
+            for k in (0, 2, 1):
+                w_out(k, g)
+            quant(0, g, 0, 512)
         sp(0, 0, 2)
         sp(0, 0, 3)
         quant_w(0)
@@ -318,44 +338,56 @@ def tile_r8convf_pa_t_kernel(tc, x, weight, out):
         fill(1)
         mm_y_half(0, 1)
         vector_pieces(1)
-        new_pair(0)
-        nc.vector.memset(pair[0][:, 0, 0, 0:1], 0.0)
+        new_pair(0, 1)
+        nc.vector.memset(pair[(0, 1)][:, 0, 0, 0:1], 0.0)
         mm_d(0, 1)
-        EXTRA = (2, 1, 0, 0)
-        AFTER = (0, 2, 2, 0)
+        EXTRA = (2, 0, 0, 0)
+        AFTER = (0, 2, 3, 0)
         MDFILL = (1, 1, 1, 1)
         for b in range(B):
             if b > 0:
-                new_pair(b)
+                new_pair(b, 1)
             gsum(b, 1)
             gsum(b, 3)
-            vdir(b, 0)
-            store(nc.sync, b, 2)
-            vdir(b, 4)
+            for d in V_DIRS:
+                new_od(b, d)
+                first_add(b, d, 0)
+            first_add(b, 0, 1)
+            second_add(b, 0, 0)
+            second_add(b, 0, 1)
+            store(nc.sync, b, 0)
             if b > 0:
+                final(b - 1, 5)
                 final(b - 1, 7)
+            store(nc.sync, b, 2)
+            first_add(b, 4, 1)
+            second_add(b, 4, 0)
+            second_add(b, 4, 1)
+            store(nc.sync, b, 4)
             store(nc.sync, b, 6)
             if b + 1 < B:
                 flush(b + 1)
                 fill(EXTRA[b])
                 quant(b + 1, 0)
-                quant(b + 1, 1)
-                second_plane(b + 1)
                 if b + 2 < B:
                     vector_pieces(b + 2)
-            if b + 1 < B:
-                gate(b, 5)
-            else:
-                new_od(b, 5)
-            new_od(b, 7)
+                quant(b + 1, 1)
+                second_plane(b + 1)
+            new_pair(b, 5)
             gsum(b, 5)
-            gsum(b, 7)
+            if b + 1 < B:
+                gsum(b, 7)
             if b + 1 < B:
                 mm_y_half(b + 1, 0)
                 mm_y_half(b + 1, 1)
-            final_pair(b)
-            final(b, 5)
+            if b + 1 == B:
+                vseven(b)
+            if b + 1 < B:
+                final_pair(b)
+            else:
+                final(b, 1)
+                final(b, 3)
             if b + 1 < B:
                 fill(AFTER[b + 1])
                 mm_d(b + 1, MDFILL[b + 1])
-        final(B - 1, 7)
+        final(B - 1, 5, 2)

@@ -32,7 +32,7 @@ PE_DIRS = (2, 6)
 V_DIRS = (0, 4)
 G_DIRS = (1, 3, 5, 7)
 PAIR = (1, 3)
-V_PIECES = (((0, 1), (0, 1, 2, 3)), ((0, 1), (0, 1)), ((0, 1), ()), ((), ()))
+V_PIECES = (((0, 1), (0, 1, 2, 3)), ((0, 1), (0,)), ((0, 1), ()), ((), ()))
 
 
 def tile_r8convf_pa_t_kernel(tc, x, weight, out):
@@ -226,11 +226,11 @@ def tile_r8convf_pa_t_kernel(tc, x, weight, out):
             acc = ps_ev.tile([P, TROWS, W], F32, name="acc", tag="ev")
             passes(acc, b, i, [(0, 0)])
             nc.scalar.copy(out=y0pad[b % 2][:, 1 + TROWS * i:1 + TROWS * (i + 1), PC:PC + W], in_=acc[:])
-            y1[(b, i)] = ps_y1.tile([P, TROWS, W], F32, name="acc1", tag="y1")
-            passes(y1[(b, i)], b, i, [(1, 0)])
             y2[(b, i)] = ps_y2.tile([P, TROWS, W], F32, name="acc2", tag="y2")
             passes(y2[(b, i)], b, i, [(2, 0)])
             nc.scalar.copy(out=y2pad[b % 2][:, 1 + TROWS * i:1 + TROWS * (i + 1), PC:PC + W], in_=y2[(b, i)][:])
+            y1[(b, i)] = ps_y1.tile([P, TROWS, W], F32, name="acc1", tag="y1")
+            passes(y1[(b, i)], b, i, [(1, 0)])
 
         def mm_d(b, nfill):
             for d in PE_DIRS:
@@ -248,12 +248,12 @@ def tile_r8convf_pa_t_kernel(tc, x, weight, out):
             else:
                 pair[(b, first)] = pairs.tile([P, 2, H, W], F32, name="pair", tag="pair")
 
-        def gsum(b, d):
+        def gsum(b, d, r=0):
             dy, dx = DIRS[d]
             nc.gpsimd.tensor_tensor(
-                out=pair[(b, 1 + d // 4 * 4)][:, d // 2 % 2, :, :],
-                in0=y0pad[b % 2][:, 1 - dy:1 - dy + H, PC - dx:PC - dx + W],
-                in1=y2pad[b % 2][:, 1 + dy:1 + dy + H, PC + dx:PC + dx + W],
+                out=pair[(b, 1 + d // 4 * 4)][:, d // 2 % 2, r:H, :],
+                in0=y0pad[b % 2][:, 1 - dy + r:1 - dy + H, PC - dx:PC - dx + W],
+                in1=y2pad[b % 2][:, 1 + dy + r:1 + dy + H, PC + dx:PC + dx + W],
                 op=ADD,
             )
 
@@ -274,39 +274,34 @@ def tile_r8convf_pa_t_kernel(tc, x, weight, out):
             t = od[(b, d)][:, r:r + TROWS, lo:lo + W - 1]
             nc.vector.tensor_tensor(out=t, in0=y2[(b, i)][:, :, lo + dx:lo + dx + W - 1], in1=t, op=ADD)
 
-        def vseven(b):
-            dy, dx = DIRS[7]
-            t = new_od(b, 7)
-            for i in range(2):
-                r = TROWS * i
-                nc.vector.tensor_tensor(
-                    out=t[:, r:r + TROWS, :],
-                    in0=y1[(b, i)][:],
-                    in1=y0pad[b % 2][:, 1 + r - dy:1 + r - dy + TROWS, PC - dx:PC - dx + W],
-                    op=ADD,
-                )
-            for i in range(2):
-                r = TROWS * i + 1
-                n = min(TROWS, H - r)
-                part = t[:, r:r + n, 0:W - 1]
-                nc.vector.tensor_tensor(out=part, in0=y2[(b, i)][:, 0:n, 1:W], in1=part, op=ADD)
-            store(nc.sync, b, 7)
+        def store_rows(b, d, r, n, t):
+            nc.sync.dma_start(
+                out=out[b, :, d, r:r + n, :].rearrange("o h w -> o (h w)"), in_=t.rearrange("p h w -> p (h w)"))
 
-        def final(b, d, stores=1):
+        def upper_seven(b):
+            dy, dx = DIRS[7]
+            t = pair[(b, 5)][:, 1, 0:TROWS, :]
+            nc.vector.tensor_tensor(
+                out=t,
+                in0=y1[(b, 0)][:],
+                in1=y0pad[b % 2][:, 1 - dy:1 - dy + TROWS, PC - dx:PC - dx + W],
+                op=ADD,
+            )
+            part = pair[(b, 5)][:, 1, 1:TROWS, 0:W - 1]
+            nc.vector.tensor_tensor(out=part, in0=y2[(b, 0)][:, 0:TROWS - 1, 1:W], in1=part, op=ADD)
+            store_rows(b, 7, 0, TROWS, t)
+
+        def final(b, d, halves=(0, 1)):
             t = pair[(b, 1 + d // 4 * 4)][:, d // 2 % 2, :, :]
-            rows = H // stores
-            for i in range(2):
+            for i in halves:
                 r = TROWS * i
                 nc.vector.tensor_tensor(
                     out=t[:, r:r + TROWS, :], in0=y1[(b, i)][:], in1=t[:, r:r + TROWS, :], op=ADD)
-                if (i + 1) * TROWS % rows == 0:
-                    r = (i + 1) * TROWS - rows
-                    nc.sync.dma_start(
-                        out=out[b, :, d, r:r + rows, :].rearrange("o h w -> o (h w)"),
-                        in_=t[:, r:r + rows, :].rearrange("p h w -> p (h w)"))
+            r = TROWS * halves[0]
+            store_rows(b, d, r, H - r, t[:, r:H, :])
 
-        def final_pair(b):
-            t = pair[(b, 1)]
+        def final_pair(b, first):
+            t = pair[(b, first)]
             for i in range(2):
                 r = TROWS * i
                 nc.vector.tensor_tensor(
@@ -316,7 +311,7 @@ def tile_r8convf_pa_t_kernel(tc, x, weight, out):
                     op=ADD,
                 )
             nc.sync.dma_start(
-                out=out[b, :, PAIR[0]:PAIR[1] + 1:2, :, :].rearrange("o d h w -> o d (h w)"),
+                out=out[b, :, first:first + 3:2, :, :].rearrange("o d h w -> o d (h w)"),
                 in_=t[:].rearrange("p d h w -> p d (h w)"),
             )
 
@@ -328,8 +323,8 @@ def tile_r8convf_pa_t_kernel(tc, x, weight, out):
         sp(0, 0, 2)
         sp(0, 0, 3)
         quant_w(0)
-        quant_w(1)
         quant_w(2)
+        quant_w(1)
         mm_y_half(0, 0)
         vp(0, 1, 2, 2)
         quant(0, 0, 512, 512)
@@ -340,8 +335,9 @@ def tile_r8convf_pa_t_kernel(tc, x, weight, out):
         vector_pieces(1)
         new_pair(0, 1)
         nc.vector.memset(pair[(0, 1)][:, 0, 0, 0:1], 0.0)
+        fill(2)
         mm_d(0, 1)
-        EXTRA = (2, 0, 0, 0)
+        EXTRA = (1, 0, 0, 0)
         AFTER = (0, 2, 3, 0)
         MDFILL = (1, 1, 1, 1)
         for b in range(B):
@@ -352,19 +348,22 @@ def tile_r8convf_pa_t_kernel(tc, x, weight, out):
             for d in V_DIRS:
                 new_od(b, d)
                 first_add(b, d, 0)
-            first_add(b, 0, 1)
             second_add(b, 0, 0)
+            first_add(b, 0, 1)
             second_add(b, 0, 1)
             store(nc.sync, b, 0)
-            if b > 0:
+            if b + 1 == B:
                 final(b - 1, 5)
                 final(b - 1, 7)
+            elif b > 0:
+                final_pair(b - 1, 5)
             store(nc.sync, b, 2)
             first_add(b, 4, 1)
             second_add(b, 4, 0)
             second_add(b, 4, 1)
             store(nc.sync, b, 4)
-            store(nc.sync, b, 6)
+            if b + 1 < B:
+                store(nc.sync, b, 6)
             if b + 1 < B:
                 flush(b + 1)
                 fill(EXTRA[b])
@@ -375,19 +374,20 @@ def tile_r8convf_pa_t_kernel(tc, x, weight, out):
                 second_plane(b + 1)
             new_pair(b, 5)
             gsum(b, 5)
-            if b + 1 < B:
-                gsum(b, 7)
+            gsum(b, 7, 0 if b + 1 < B else TROWS)
             if b + 1 < B:
                 mm_y_half(b + 1, 0)
                 mm_y_half(b + 1, 1)
             if b + 1 == B:
-                vseven(b)
+                upper_seven(b)
             if b + 1 < B:
-                final_pair(b)
+                final_pair(b, 1)
             else:
                 final(b, 1)
+                store(nc.sync, b, 6)
                 final(b, 3)
             if b + 1 < B:
                 fill(AFTER[b + 1])
                 mm_d(b + 1, MDFILL[b + 1])
-        final(B - 1, 5, 2)
+        final(B - 1, 5)
+        final(B - 1, 7, (1,))

from contextlib import ExitStack

import concourse.mybir as mybir
from concourse.masks import make_identity

FP8X4 = mybir.dt.float8_e4m3fn_x4
BF16 = mybir.dt.bfloat16
F32 = mybir.dt.float32
U32 = mybir.dt.uint32
U8 = mybir.dt.uint8
I32 = mybir.dt.int32
ADD = mybir.AluOpType.add

B, C, H, W, O, K = 4, 1024, 32, 32, 128, 3
P = 128
PASSES = 2
PIX = H * W
DIRS = [(0, 1), (1, 1), (1, 0), (1, -1), (0, -1), (-1, -1), (-1, 0), (-1, 1)]
FLOPS = 2 * K * O * C * B * H * W

GAP = 64
PITCH = PIX + GAP
NBLK = B * PASSES
FLAT = NBLK * PITCH + GAP
TROWS = 16
PIECE = 256
RUN = 4
PW = 40
PC = 4

PE_DIRS = (2, 6)
V_DIRS = (0, 4)
G_DIRS = (1, 3, 5, 7)
PAIR = (1, 3)
V_PIECES = (((0, 1), (0, 1, 2, 3)), ((0, 1), (0,)), ((0, 1), ()), ((), ()))


def tile_r8convf_pa_t_kernel(tc, x, weight, out):
    nc = tc.nc
    with ExitStack() as ctx:
        keep = ctx.enter_context(tc.tile_pool(name="keep", bufs=1))
        raws = ctx.enter_context(tc.tile_pool(name="raws", bufs=6))
        stage = ctx.enter_context(tc.tile_pool(name="stage", bufs=1))
        heads = ctx.enter_context(tc.tile_pool(name="heads", bufs=1))
        outs = ctx.enter_context(tc.tile_pool(name="outs", bufs=7))
        pairs = ctx.enter_context(tc.tile_pool(name="pairs", bufs=3))
        ps_y1 = ctx.enter_context(tc.psum_pool(name="ps_y1", bufs=4))
        ps_y2 = ctx.enter_context(tc.psum_pool(name="ps_y2", bufs=2))
        ps_ev = ctx.enter_context(tc.psum_pool(name="ps_ev", bufs=2))
        ctx.enter_context(tc.manual_schedule())

        codes = keep.tile([P, FLAT], U32, name="codes", align_bytes=64)
        sc_a = keep.tile([P, FLAT], U8, name="sc_a", align_bytes=64)
        sc_b = keep.tile([P, FLAT], U8, name="sc_b", align_bytes=64)
        y0pad = [keep.tile([P, H + 2, PW], F32, name="y0pad%d" % s, align_bytes=64) for s in range(2)]
        y2pad = [keep.tile([P, H + 2, PW], F32, name="y2pad%d" % s, align_bytes=64) for s in range(2)]
        w_sb = keep.tile([P, C * K], BF16, name="w_sb")
        wg = [keep.tile([P, PASSES, P, 4], BF16, name="wg%d" % k, align_bytes=64) for k in range(K)]
        wq = [keep.tile([P, PASSES * P], U32, name="wq%d" % k, align_bytes=64) for k in range(K)]
        ws = [keep.tile([P, PASSES * P], U8, name="ws%d" % k, align_bytes=64) for k in range(K)]
        ident = keep.tile([P, P], BF16, name="ident")
        raw = {}
        grouped = {}

        def base(b, g):
            return (PASSES * b + g) * PITCH + GAP

        def load_part(b, lo, n, gs=(0, 1)):
            for g in gs:
                if b == 0:
                    raw[(b, g, lo)] = heads.tile([P, 4, n], BF16, name="head", tag="head%d%d" % (g, lo))
                    dst = raw[(b, g, lo)][:]
                else:
                    raw[(b, g)] = raws.tile([P, 4, PIX], BF16, name="raw", tag="raw")
                    dst = raw[(b, g)][:]
                nc.sync.dma_start(
                    out=dst,
                    in_=x[b, 512 * g:512 * (g + 1), :, :].rearrange("(p j) h w -> p j (h w)", j=4)[:, :, lo:lo + n],
                )

        def load(b, halves):
            for h in range(halves):
                load_part(b, h * (PIX // halves), PIX // halves)

        for g in range(PASSES):
            nc.sync.dma_start(
                out=w_sb[:, C * K // 2 * g:C * K // 2 * (g + 1)],
                in_=weight[:, C // 2 * g:C // 2 * (g + 1), :].rearrange("o c k -> o (c k)"))
            load_part(0, 0, PIX // 2, (g,))
        load_part(0, PIX // 2, PIX // 2)
        load(1, 1)
        load(2, 1)
        load(3, 1)

        make_identity(nc, ident[:])
        nc.vector.memset(codes[:, 0:NBLK * PITCH].rearrange("p (n c) -> p n c", c=PITCH)[:, :, 0:GAP].bitcast(I32), 0)
        nc.vector.memset(codes[:, NBLK * PITCH:FLAT].bitcast(I32), 0)
        nc.vector.memset(sc_b[:, 32:32 + NBLK * PITCH].rearrange("p (n c) -> p n c", c=PITCH)[:, :, 0:GAP].bitcast(I32), 0)
        nc.vector.memset(sc_b[:, 32 + NBLK * PITCH:FLAT].bitcast(I32), 0)
        for t in y0pad + y2pad:
            nc.gpsimd.memset(t[:, 0:H + 2:H + 1, :], 0.0)
            nc.gpsimd.memset(t[:, :, PC - 1:PC + W + 1:W + 1], 0.0)

        w_view = w_sb[:].rearrange("o (g p t k) -> o k g t p", g=PASSES, p=P, t=4, k=K)
        wt = {}
        for g in range(PASSES):
            for k in (0, 2, 1):
                pool, tag = (ps_y1, "y1") if g == 0 or k == 0 else (ps_ev, "ev")
                wt[(k, g)] = pool.tile([P, 4, P], BF16, name="wt", tag=tag)
                for t in range(4):
                    nc.tensor.transpose(wt[(k, g)][:, t, :], w_view[:, k, g, t, :], ident[:])

        def w_out(k, g):
            nc.scalar.copy(out=wg[k][:, g, :, :], in_=wt[(k, g)][:].rearrange("p t o -> p o t"))

        def quant_w(k):
            nc.vector.quantize_mx(
                out=wq[k][:].bitcast(FP8X4), scales=ws[k][:], in_=wg[k][:].rearrange("p g o t -> p (g o t)"))

        def piece(engine_copy, b, g, q, n):
            if (b, g) not in grouped:
                grouped[(b, g)] = stage.tile([P, PIX, 4], BF16, name="grouped", tag="s%d%d" % (b % 2, g), align_bytes=64)
            lo = PIECE * q
            if b == 0:
                first = lo // (PIX // 2) * (PIX // 2)
                src = raw[(b, g, first)][:, :, lo - first:lo - first + PIECE * n]
            else:
                src = raw[(b, g)][:, :, lo:lo + PIECE * n]
            engine_copy(
                out=grouped[(b, g)][:, lo:lo + PIECE * n, :].rearrange("p (c i) t -> p c t i", i=RUN),
                in_=src.rearrange("p t (c i) -> p c t i", i=RUN),
            )

        todo = {(b, g): [q for q in range(4)] for b in range(B) for g in range(PASSES)}
        order = [(b, g) for b in range(B) for g in range(PASSES)]

        def vp(b, g, q, n):
            for j in range(n):
                todo[(b, g)].remove(q + j)
            piece(nc.vector.tensor_copy, b, g, q, n)

        def sp(b, g, q):
            todo[(b, g)].remove(q)
            piece(nc.scalar.copy, b, g, q, 1)

        vshare = {(b, g): list(V_PIECES[b][g]) for b in range(B) for g in range(PASSES)}

        def vector_pieces(b):
            for g in range(PASSES):
                if len(vshare[(b, g)]) > 0:
                    vp(b, g, vshare[(b, g)][0], len(vshare[(b, g)]))

        def s_next():
            for bg in order:
                for q in todo[bg]:
                    if q not in vshare[bg]:
                        return (bg[0], bg[1], q)
            return None

        def fill(n):
            for r in range(n):
                nx = s_next()
                if nx is not None:
                    sp(nx[0], nx[1], nx[2])

        def flush(b):
            nx = s_next()
            while nx is not None and nx[0] <= b:
                sp(nx[0], nx[1], nx[2])
                nx = s_next()

        def quant(b, g, lo=0, n=PIX):
            c0 = base(b, g) + lo
            nc.vector.quantize_mx(
                out=codes[:, c0:c0 + n].bitcast(FP8X4),
                scales=sc_a[:, c0:c0 + n],
                in_=grouped[(b, g)][:, lo:lo + n, :].rearrange("p n t -> p (n t)"),
            )

        def second_plane(b):
            bs = base(b, 0) - GAP
            moves = [(nc.vector.tensor_copy, 0, P)] if b == 0 else [(nc.sync.dma_start, 32 * q, 32 * q + 4) for q in range(4)]
            for mover, lo, hi in moves:
                mover(
                    out=sc_b[lo:hi, bs + 32:bs + 32 + PASSES * PITCH].rearrange("p (g c) -> p g c", c=PITCH)[:, :, GAP:GAP + PIX].bitcast(I32),
                    in_=sc_a[lo:hi, bs:bs + PASSES * PITCH].rearrange("p (g c) -> p g c", c=PITCH)[:, :, GAP:GAP + PIX].bitcast(I32),
                )

        def passes(acc, b, i, taps):
            n = len(taps) * PASSES
            j = 0
            for k, s in taps:
                for g in range(PASSES):
                    c0 = base(b, g) + W * (TROWS * i + s)
                    if s == 0:
                        plane = sc_a[:, c0:c0 + 512]
                    else:
                        plane = sc_b[:, c0 + 32:c0 + 32 + 512]
                    nc.tensor.matmul_mx(
                        out=acc[:].rearrange("p h w -> p (h w)"),
                        lhsT=wq[k][:, P * g:P * (g + 1)].bitcast(FP8X4),
                        lhsT_scale=ws[k][:, P * g:P * (g + 1)],
                        rhs=codes[:, c0:c0 + 512].bitcast(FP8X4),
                        rhs_scale=plane,
                        start=(j == 0),
                        stop=(j == n - 1),
                    )
                    j += 1

        od = {}
        pair = {}
        y1 = {}
        y2 = {}

        def new_od(b, d):
            od[(b, d)] = outs.tile([P, H, W], F32, name="od", tag="od")
            return od[(b, d)]

        def store(queue, b, d):
            queue.dma_start(
                out=out[b, :, d, :, :].rearrange("o h w -> o (h w)"),
                in_=od[(b, d)][:].rearrange("p h w -> p (h w)"),
            )

        def mm_y_half(b, i):
            acc = ps_ev.tile([P, TROWS, W], F32, name="acc", tag="ev")
            passes(acc, b, i, [(0, 0)])
            nc.scalar.copy(out=y0pad[b % 2][:, 1 + TROWS * i:1 + TROWS * (i + 1), PC:PC + W], in_=acc[:])
            y2[(b, i)] = ps_y2.tile([P, TROWS, W], F32, name="acc2", tag="y2")
            passes(y2[(b, i)], b, i, [(2, 0)])
            nc.scalar.copy(out=y2pad[b % 2][:, 1 + TROWS * i:1 + TROWS * (i + 1), PC:PC + W], in_=y2[(b, i)][:])
            y1[(b, i)] = ps_y1.tile([P, TROWS, W], F32, name="acc1", tag="y1")
            passes(y1[(b, i)], b, i, [(1, 0)])

        def mm_d(b, nfill):
            for d in PE_DIRS:
                dy = DIRS[d][0]
                t = new_od(b, d)
                for i in range(2):
                    acc = ps_ev.tile([P, TROWS, W], F32, name="acc", tag="ev")
                    passes(acc, b, i, [(1, 0), (0, -dy), (2, dy)])
                    nc.scalar.copy(out=t[:, TROWS * i:TROWS * (i + 1), :], in_=acc[:])
                    fill(nfill)

        def new_pair(b, first):
            if first == 5 and b + 1 < B:
                pair[(b, first)] = stage.tile([P, 2, H, W], F32, name="late", tag="s%d1" % ((b + 1) % 2), align_bytes=64)
            else:
                pair[(b, first)] = pairs.tile([P, 2, H, W], F32, name="pair", tag="pair")

        def gsum(b, d, r=0):
            dy, dx = DIRS[d]
            nc.gpsimd.tensor_tensor(
                out=pair[(b, 1 + d // 4 * 4)][:, d // 2 % 2, r:H, :],
                in0=y0pad[b % 2][:, 1 - dy + r:1 - dy + H, PC - dx:PC - dx + W],
                in1=y2pad[b % 2][:, 1 + dy + r:1 + dy + H, PC + dx:PC + dx + W],
                op=ADD,
            )

        def first_add(b, d, i):
            r = TROWS * i
            dx = DIRS[d][1]
            nc.vector.tensor_tensor(
                out=od[(b, d)][:, r:r + TROWS, :],
                in0=y1[(b, i)][:],
                in1=y0pad[b % 2][:, 1 + r:1 + r + TROWS, PC - dx:PC - dx + W],
                op=ADD,
            )

        def second_add(b, d, i):
            r = TROWS * i
            dx = DIRS[d][1]
            lo = max(0, -dx)
            t = od[(b, d)][:, r:r + TROWS, lo:lo + W - 1]
            nc.vector.tensor_tensor(out=t, in0=y2[(b, i)][:, :, lo + dx:lo + dx + W - 1], in1=t, op=ADD)

        def store_rows(b, d, r, n, t):
            nc.sync.dma_start(
                out=out[b, :, d, r:r + n, :].rearrange("o h w -> o (h w)"), in_=t.rearrange("p h w -> p (h w)"))

        def upper_seven(b):
            dy, dx = DIRS[7]
            t = pair[(b, 5)][:, 1, 0:TROWS, :]
            nc.vector.tensor_tensor(
                out=t,
                in0=y1[(b, 0)][:],
                in1=y0pad[b % 2][:, 1 - dy:1 - dy + TROWS, PC - dx:PC - dx + W],
                op=ADD,
            )
            part = pair[(b, 5)][:, 1, 1:TROWS, 0:W - 1]
            nc.vector.tensor_tensor(out=part, in0=y2[(b, 0)][:, 0:TROWS - 1, 1:W], in1=part, op=ADD)
            store_rows(b, 7, 0, TROWS, t)

        def final(b, d, halves=(0, 1)):
            t = pair[(b, 1 + d // 4 * 4)][:, d // 2 % 2, :, :]
            for i in halves:
                r = TROWS * i
                nc.vector.tensor_tensor(
                    out=t[:, r:r + TROWS, :], in0=y1[(b, i)][:], in1=t[:, r:r + TROWS, :], op=ADD)
            r = TROWS * halves[0]
            store_rows(b, d, r, H - r, t[:, r:H, :])

        def final_pair(b, first):
            t = pair[(b, first)]
            for i in range(2):
                r = TROWS * i
                nc.vector.tensor_tensor(
                    out=t[:, :, r:r + TROWS, :],
                    in0=y1[(b, i)][:].unsqueeze(1).to_broadcast([P, 2, TROWS, W]),
                    in1=t[:, :, r:r + TROWS, :],
                    op=ADD,
                )
            nc.sync.dma_start(
                out=out[b, :, first:first + 3:2, :, :].rearrange("o d h w -> o d (h w)"),
                in_=t[:].rearrange("p d h w -> p d (h w)"),
            )

        for g in range(PASSES):
            vp(0, g, 0, 2)
            for k in (0, 2, 1):
                w_out(k, g)
            quant(0, g, 0, 512)
        sp(0, 0, 2)
        sp(0, 0, 3)
        quant_w(0)
        quant_w(2)
        quant_w(1)
        mm_y_half(0, 0)
        vp(0, 1, 2, 2)
        quant(0, 0, 512, 512)
        quant(0, 1, 512, 512)
        second_plane(0)
        fill(1)
        mm_y_half(0, 1)
        vector_pieces(1)
        new_pair(0, 1)
        nc.vector.memset(pair[(0, 1)][:, 0, 0, 0:1], 0.0)
        fill(2)
        mm_d(0, 1)
        EXTRA = (1, 0, 0, 0)
        AFTER = (0, 2, 3, 0)
        MDFILL = (1, 1, 1, 1)
        for b in range(B):
            if b > 0:
                new_pair(b, 1)
            gsum(b, 1)
            gsum(b, 3)
            for d in V_DIRS:
                new_od(b, d)
                first_add(b, d, 0)
            second_add(b, 0, 0)
            first_add(b, 0, 1)
            second_add(b, 0, 1)
            store(nc.sync, b, 0)
            if b + 1 == B:
                final(b - 1, 5)
                final(b - 1, 7)
            elif b > 0:
                final_pair(b - 1, 5)
            store(nc.sync, b, 2)
            first_add(b, 4, 1)
            second_add(b, 4, 0)
            second_add(b, 4, 1)
            store(nc.sync, b, 4)
            if b + 1 < B:
                store(nc.sync, b, 6)
            if b + 1 < B:
                flush(b + 1)
                fill(EXTRA[b])
                quant(b + 1, 0)
                if b + 2 < B:
                    vector_pieces(b + 2)
                quant(b + 1, 1)
                second_plane(b + 1)
            new_pair(b, 5)
            gsum(b, 5)
            gsum(b, 7, 0 if b + 1 < B else TROWS)
            if b + 1 < B:
                mm_y_half(b + 1, 0)
                mm_y_half(b + 1, 1)
            if b + 1 == B:
                upper_seven(b)
            if b + 1 < B:
                final_pair(b, 1)
            else:
                final(b, 1)
                store(nc.sync, b, 6)
                final(b, 3)
            if b + 1 < B:
                fill(AFTER[b + 1])
                mm_d(b + 1, MDFILL[b + 1])
        final(B - 1, 5)
        final(B - 1, 7, (1,))
